import numpy as np
import ml_dtypes


def mxq(x, axis, fmt="e4m3"):
    dtype, down = {"e4m3": (ml_dtypes.float8_e4m3fn, 7), "e5m2": (ml_dtypes.float8_e5m2, 14)}[fmt]
    v = np.moveaxis(np.asarray(x, np.float32).astype(ml_dtypes.bfloat16).astype(np.float64), axis, -1)
    blocks = v.reshape(v.shape[:-1] + (-1, 32))
    amax = np.abs(blocks).max(-1, keepdims=True)
    byte = np.maximum(np.where(amax > 0, np.frexp(amax)[1] - 1 + 127, 0) - down, 1)
    scale = np.exp2(byte - 127.0)
    codes = (blocks / scale).astype(np.float32).astype(dtype).astype(np.float64)
    return np.moveaxis((codes * scale).reshape(v.shape), -1, axis)


WIDE = False


def mx_kscale(k):
    if not WIDE:
        return np.ones(k)
    levels = np.array([10, -10, 5, -5, 0])
    a = np.random.permutation(np.resize(levels, k // 512 * 4)).reshape(k // 512, 4)
    idx = np.arange(k)
    return np.exp2(a[idx // 512, idx % 128 // 32])


BF16 = ml_dtypes.bfloat16


def bf(x):
    return np.asarray(x, np.float32).astype(BF16)


def f64(x):
    return np.asarray(x).astype(np.float64)


B, N, C0, C1, C2, O0, O1, O2 = 256, 16, 256, 512, 128, 512, 256, 512
P = C0 + C1
K = P + 2 * C2


def sigmoid(v):
    return 1.0 / (1.0 + np.exp(-v))


def setup_inputs():
    s = mx_kscale(K)[:P]
    lo = 0.4 * np.random.random((B, N, 1, C2))
    hi = 1.0 - 0.4 * np.random.random((B, N, 1, C2))
    x2 = lo + (hi - lo) * np.random.random((B, N, N, C2))
    i = np.arange(N)
    x2[:, i, i, :] = np.random.random((B, N, C2)) < 0.5
    w = np.random.standard_normal((K, O1)) * 2.0 / np.sqrt(K)
    w[:P] = w[:P] / s[:, None]
    return {"x0": bf(np.random.random((B, C0)) * s[:C0]),
            "x1": bf(np.random.random((B, N, C1)) * s[C0:]),
            "x2": bf(x2),
            "W1": bf(w),
            "b1": bf(np.random.standard_normal(O1) * 0.3)}


def reference(x0, x1, x2, W1, b1):
    x0, x1, x2 = f64(x0), f64(x1), f64(x2)
    e0 = np.broadcast_to(x0[:, None, :], (B, N, C0))
    diag = np.eye(N, dtype=bool)[None, :, :, None]
    rmax = np.where(diag, 0.0, x2).max(axis=2)
    rmin = np.where(diag, 1.0, x2).min(axis=2)
    f1 = np.concatenate([e0, x1, rmax, rmin], axis=-1)
    return sigmoid((mxq(f1, 2, "e4m3") @ mxq(f64(W1), 0, "e4m3")) + f64(b1))

@@ -1,0 +1,327 @@
+from contextlib import ExitStack
+
+import concourse.bass as bass
+import concourse.mybir as mybir
+import concourse.tile as tile
+from concourse.masks import make_identity
+
+F32 = mybir.dt.float32
+BF16 = mybir.dt.bfloat16
+U32 = mybir.dt.uint32
+U8 = mybir.dt.uint8
+I32 = mybir.dt.int32
+FP8X4 = mybir.dt.float8_e4m3fn_x4
+ALU = mybir.AluOpType
+ACTF = mybir.ActivationFunctionType
+
+P = 128
+B, N, C0, C1, C2, O1 = 256, 16, 256, 512, 128, 256
+K = C0 + C1 + 2 * C2
+E = N - 1
+RUN = N * C2
+REP = 2
+
+UNITS = (
+    (0, 0, 4, ((0, 2), (2, 4))),
+    (0, 4, 4, ((4, 8),)),
+    (0, 8, 4, ((8, 12),)),
+    (0, 12, 4, ((12, 16),)),
+    (1, 0, 4, ((0, 4),)),
+    (1, 4, 4, ((4, 8),)),
+    (1, 8, 4, ((8, 12),)),
+    (1, 12, 2, ((12, 14),)),
+    (1, 14, 2, ((14, 16),)),
+)
+NU = 9
+assert len(UNITS) == NU
+
+FLOPS = 2 * B * N * K * O1
+BYTES = 2 * (B * C0 + B * N * C1 + B * N * E * C2 + K * O1 + O1) + 4 * B * N * O1
+
+S_X1, S_X0, S_LO, S_HI = 0, 1, 2, 3
+
+
+def tile_differentiablelogicmachine_pb_t_kernel(tc, x0, x1, x2, W1, b1, out):
+    nc = tc.nc
+    with ExitStack() as ctx:
+        const = ctx.enter_context(tc.tile_pool(name="const", bufs=1))
+        big = ctx.enter_context(tc.tile_pool(name="big", bufs=1))
+        x1p = ctx.enter_context(tc.tile_pool(name="x1p", bufs=4))
+        work = ctx.enter_context(tc.tile_pool(name="work", bufs=2))
+        ps_init = ctx.enter_context(tc.psum_pool(name="ps_init", bufs=1))
+        ps_tx = ctx.enter_context(tc.psum_pool(name="ps_tx", bufs=2))
+        ps_tr = ctx.enter_context(tc.psum_pool(name="ps_tr", bufs=1))
+        ps_acc = ctx.enter_context(tc.psum_pool(name="ps_acc", bufs=2))
+        ps_ot = ctx.enter_context(tc.psum_pool(name="ps_ot", bufs=2))
+        ctx.enter_context(tc.manual_schedule())
+
+        wraw = const.tile([P, 4, 4, O1], BF16, name="wraw", tag="wraw")
+        wgrp = const.tile([P, 4, O1, 4], BF16, name="wgrp", tag="wgrp", align_bytes=64)
+        wcod = const.tile([P, 4 * O1], U32, name="wcod", tag="wcod", align_bytes=64)
+        wscl = const.tile([P, 4 * O1], U8, name="wscl", tag="wscl", align_bytes=64)
+        x0sb = const.tile([P, 2, C0], BF16, name="x0sb", tag="x0sb")
+        g0 = const.tile([P, 2, REP, P, 2], F32, name="g0", tag="g0", align_bytes=64)
+        x0cod = const.tile([P, 2 * REP * P], U32, name="x0cod", tag="x0cod", align_bytes=64)
+        x0scl = const.tile([P, 2 * REP * P], U8, name="x0scl", tag="x0scl", align_bytes=64)
+        bz = const.tile([P, P], BF16, name="bz", tag="bz")
+        bias = const.tile([P, 2], F32, name="bias", tag="bias")
+        warm = const.tile([P, 2], F32, name="warm", tag="warm")
+        idf = const.tile([P, P], F32, name="idf", tag="idf")
+        idb = const.tile([P, P], BF16, name="idb", tag="idb")
+
+        nc.vector.memset(warm[:], 0.0)
+        nc.vector.memset(bz[:], 0.0)
+        nc.vector.memset(wraw[:, S_X0, 2:4, :], 0.0)
+        nc.vector.memset(wraw[64:128, S_LO, :, :], 0.0)
+        nc.vector.memset(wraw[0:64, S_HI, :, :], 0.0)
+        nc.vector.memset(g0[:], 0.0)
+        make_identity(nc, idf[:])
+        make_identity(nc, idb[:])
+        nc.scalar.activation(out=warm[:, 1:2], in_=warm[:, 0:1], func=ACTF.Sigmoid)
+
+        xt = [big.tile([P, N, E, C2], BF16, name="xt%d" % h, tag="xt%d" % h) for h in range(2)]
+
+        def load_x2(u):
+            h = UNITS[u][0]
+            for a, b in UNITS[u][3]:
+                g_lo = (E * a + N - 1) // N
+                g_hi = (E * b + N - 1) // N
+                src = x2[h * P:(h + 1) * P].rearrange("b i j c -> b (i j c)")[:, C2:N * N * C2]
+                src = src.rearrange("b (g r) -> b g r", r=RUN + C2)[:, g_lo:g_hi, 0:RUN]
+                dst = xt[h][:].rearrange("p i e c -> p (i e c)")[:, g_lo * RUN:g_hi * RUN]
+                nc.sync.dma_start(out=dst.rearrange("p (g r) -> p g r", r=RUN), in_=src)
+
+        x1t = {}
+
+        def load_x1(u):
+            h, i0, nr = UNITS[u][0:3]
+            t = x1p.tile([P, nr * C1], BF16, name="x1t", tag="x1t")
+            nc.sync.dma_start(
+                out=t[:].rearrange("p (i k) -> p i k", k=C1),
+                in_=x1[h * P:(h + 1) * P, i0:i0 + nr, :],
+            )
+            x1t[u] = t
+
+        load_x2(0)
+        nc.sync.dma_start(out=wraw[:, S_X1, :, :], in_=W1[C0:C0 + C1, :].rearrange("(p j) o -> p j o", j=4))
+        nc.sync.dma_start(out=wraw[:, S_X0, 0:2, :], in_=W1[0:C0, :].rearrange("(p e) o -> p e o", e=2))
+        wr_src = W1[C0 + C1:K, :].rearrange("(u p e) o -> p u (e o)", u=2, e=2)
+        nc.sync.dma_start(out=wraw[0:64, S_LO, :, :].rearrange("p (u e) o -> p u (e o)", u=2), in_=wr_src)
+        nc.sync.dma_start(out=wraw[64:128, S_HI, :, :].rearrange("p (u e) o -> p u (e o)", u=2), in_=wr_src)
+        nc.sync.dma_start(out=x0sb[:], in_=x0.rearrange("(h b) k -> b h k", h=2))
+        nc.sync.dma_start(out=bz[0:2, :], in_=b1.rearrange("(r c) -> r c", r=2))
+        load_x1(0)
+        load_x2(1)
+        load_x1(1)
+        load_x2(2)
+        load_x1(2)
+        load_x2(3)
+        load_x1(3)
+
+        rmax, rmin, m1s = {}, {}, {}
+        tt = nc.vector.tensor_tensor
+
+        def level1(u, g):
+            h = UNITS[u][0]
+            a, b = UNITS[u][3][g]
+            x = xt[h]
+            m1 = work.tile([P, b - a, 7, C2], BF16, name="m1", tag="m1")
+            m1s[(u, g)] = m1
+            tt(out=m1[:], in0=x[:, a:b, 0:7, :], in1=x[:, a:b, 8:15, :], op=ALU.max)
+            tt(out=x[:, a:b, 0:7, :], in0=x[:, a:b, 0:7, :], in1=x[:, a:b, 8:15, :], op=ALU.min)
+
+        def levels234(u, g):
+            h, i0 = UNITS[u][0:2]
+            a, b = UNITS[u][3][g]
+            x = xt[h]
+            m1 = m1s[(u, g)]
+            rx, rn = rmax[u], rmin[u]
+            tt(out=m1[:, :, 0:3, :], in0=m1[:, :, 0:3, :], in1=m1[:, :, 3:6, :], op=ALU.max)
+            tt(out=x[:, a:b, 0:4, :], in0=x[:, a:b, 0:4, :], in1=x[:, a:b, 4:8, :], op=ALU.min)
+            tt(out=m1[:, :, 3, :], in0=m1[:, :, 6, :], in1=x[:, a:b, 7, :], op=ALU.max)
+            tt(out=x[:, a:b, 0:2, :], in0=x[:, a:b, 0:2, :], in1=x[:, a:b, 2:4, :], op=ALU.min)
+            tt(out=m1[:, :, 0:2, :], in0=m1[:, :, 0:2, :], in1=m1[:, :, 2:4, :], op=ALU.max)
+            tt(out=rn[:, a - i0:b - i0, :], in0=x[:, a:b, 0, :], in1=x[:, a:b, 1, :], op=ALU.min)
+            tt(out=rx[:, a - i0:b - i0, :], in0=m1[:, :, 0, :], in1=m1[:, :, 1, :], op=ALU.max)
+
+        def tree_a(u):
+            level1(u, 0)
+
+        def tree_b(u):
+            nr = UNITS[u][2]
+            rx = work.tile([P, nr, C2], BF16, name="rx", tag="rx")
+            rn = work.tile([P, nr, C2], BF16, name="rn", tag="rn")
+            rmax[u], rmin[u] = rx, rn
+            levels234(u, 0)
+            for g in range(1, len(UNITS[u][3])):
+                level1(u, g)
+                levels234(u, g)
+            nc.vector.tensor_scalar_min(out=rn[:], in0=rn[:], scalar1=1.0)
+            nc.vector.tensor_scalar_max(out=rx[:], in0=rx[:], scalar1=0.0)
+
+        g1s, x1cs = {}, {}
+
+        def tx1(u):
+            npr = UNITS[u][2] // 2
+            words = x1t[u][:].bitcast(F32)
+            g1 = work.tile([P, 2, npr, P, 2], F32, name="g1", tag="g1", align_bytes=64)
+            g1s[u] = g1
+            for par in range(2):
+                bank = ps_tx.tile([P, npr, 2, P], F32, name="tx", tag="tx")
+                for pr in range(npr):
+                    il = 2 * pr + par
+                    for w in range(2):
+                        nc.tensor.transpose(
+                            bank[:, pr, w, :],
+                            words[:, il * (C1 // 2) + w:(il + 1) * (C1 // 2):2],
+                            idf[:],
+                        )
+                nc.scalar.copy(out=g1[:, par], in_=bank[:].rearrange("p r w b -> p r b w"))
+
+        def qx1(u):
+            ncol = UNITS[u][2] // 2 * P
+            cod = work.tile([P, 2 * ncol], U32, name="x1cod", tag="x1cod", align_bytes=64)
+            scl = work.tile([P, 2 * ncol], U8, name="x1scl", tag="x1scl", align_bytes=64)
+            x1cs[u] = (cod, scl)
+            nc.vector.quantize_mx(
+                out=cod[:].bitcast(FP8X4),
+                scales=scl[:],
+                in_=g1s[u][:].rearrange("p a r b w -> p (a r b w)").bitcast(BF16),
+            )
+
+        gts, tcs = {}, {}
+
+        def tr(u):
+            npr = UNITS[u][2] // 2
+            bank = ps_tr.tile([P, npr, 2, P], F32, name="trb", tag="trb")
+            srcs = (rmax[u], rmin[u])
+            for pr in range(npr):
+                for w in range(2):
+                    words = srcs[w][:].rearrange("p i c -> p (i c)").bitcast(F32)
+                    nc.tensor.transpose(bank[:, pr, w, :], words[:, pr * P:(pr + 1) * P], idf[:])
+            gt = work.tile([P, npr, P, 2], F32, name="gt", tag="gt", align_bytes=64)
+            gts[u] = gt
+            nc.scalar.copy(out=gt[:], in_=bank[:].rearrange("p r w b -> p r b w"))
+
+        def qr(u):
+            ncol = UNITS[u][2] // 2 * P
+            cod = work.tile([P, ncol], U32, name="rcod", tag="rcod", align_bytes=64)
+            scl = work.tile([P, ncol], U8, name="rscl", tag="rscl", align_bytes=64)
+            tcs[u] = (cod, scl)
+            nc.vector.quantize_mx(
+                out=cod[:].bitcast(FP8X4),
+                scales=scl[:],
+                in_=gts[u][:].rearrange("p r b w -> p (r b w)").bitcast(BF16),
+            )
+
+        sig, accs = {}, {}
+
+        def mx_pass(u, oh, par, kind):
+            h = UNITS[u][0]
+            ncol = UNITS[u][2] // 2 * P
+            if kind == 0:
+                slot = S_X1
+                cod = x1cs[u][0][:, par * ncol:(par + 1) * ncol]
+                scl = x1cs[u][1][:, par * ncol:(par + 1) * ncol]
+            elif kind == 1:
+                slot = S_X0
+                cod = x0cod[:, h * REP * P:h * REP * P + ncol]
+                scl = x0scl[:, h * REP * P:h * REP * P + ncol]
+            else:
+                slot = S_LO + par
+                cod = tcs[u][0][:]
+                scl = tcs[u][1][:]
+            cols = slice(slot * O1 + oh * P, slot * O1 + (oh + 1) * P)
+            nc.tensor.matmul_mx(
+                out=accs[(u, oh)][:, par, :],
+                lhsT=wcod[:, cols].bitcast(FP8X4),
+                lhsT_scale=wscl[:, cols],
+                rhs=cod.bitcast(FP8X4),
+                rhs_scale=scl,
+                start=(kind == 0),
+                stop=(kind == 2),
+            )
+
+        def mx_pre(u):
+            ncol = UNITS[u][2] // 2 * P
+            for oh in range(2):
+                accs[(u, oh)] = ps_acc.tile([P, 2, ncol], F32, name="acc", tag="acc")
+                mx_pass(u, oh, 0, 0)
+                mx_pass(u, oh, 0, 1)
+
+        def mx_post(u):
+            npr = UNITS[u][2] // 2
+            for oh in range(2):
+                mx_pass(u, oh, 0, 2)
+                for kind in range(3):
+                    mx_pass(u, oh, 1, kind)
+                s = work.tile([P, 2, npr, P], F32, name="sig%d" % oh, tag="sig%d" % oh)
+                sig[(u, oh)] = s
+                nc.scalar.activation(
+                    out=s[:].rearrange("p a r b -> p (a r b)"),
+                    in_=accs[(u, oh)][:].rearrange("p a n -> p (a n)"),
+                    func=ACTF.Sigmoid,
+                    bias=bias[:, oh:oh + 1],
+                    scale=1.0,
+                )
+
+        def fin(u):
+            h, i0, nr = UNITS[u][0:3]
+            o = work.tile([P, nr, O1], F32, name="osb", tag="osb")
+            for pr in range(nr // 2):
+                bank = ps_ot.tile([P, 2, 2, P], F32, name="ot", tag="ot")
+                for par in range(2):
+                    for oh in range(2):
+                        nc.tensor.transpose(bank[:, par, oh, :], sig[(u, oh)][:, par, pr, :], idf[:])
+                nc.scalar.copy(
+                    out=o[:, 2 * pr:2 * pr + 2, :].rearrange("p i o -> p (i o)"),
+                    in_=bank[:].rearrange("p a h o -> p (a h o)"),
+                )
+            nc.scalar.dma_start(out=out[h * P:(h + 1) * P, i0:i0 + nr, :], in_=o[:])
+
+        for s in range(4):
+            nc.scalar.copy(out=wgrp[:, s], in_=wraw[:, s].rearrange("p j o -> p o j"))
+        pb = ps_tr.tile([P, P], BF16, name="pb", tag="trb")
+        nc.tensor.transpose(pb[:], bz[:], idb[:])
+        nc.scalar.copy(out=bias[:], in_=pb[:, 0:2])
+        p0 = ps_init.tile([P, 2, P], F32, name="p0", tag="init")
+        for h in range(2):
+            nc.tensor.transpose(p0[:, h, :], x0sb[:, h, :].bitcast(F32), idf[:])
+        for rep in range(REP):
+            nc.scalar.copy(out=g0[:, :, rep, :, 0], in_=p0[:])
+
+        tree_a(0)
+        tree_b(0)
+        for u in range(2):
+            tx1(u)
+            load_x2(u + 4)
+            load_x1(u + 4)
+
+        for u in range(NU):
+            tr(u)
+            if u + 2 < NU:
+                tx1(u + 2)
+                if u + 6 < NU:
+                    load_x2(u + 6)
+                    load_x1(u + 6)
+            if u + 1 < NU:
+                tree_a(u + 1)
+            if u == 0:
+                nc.vector.quantize_mx(
+                    out=wcod[:].bitcast(FP8X4),
+                    scales=wscl[:],
+                    in_=wgrp[:].rearrange("p s o j -> p (s o j)"),
+                )
+                nc.vector.quantize_mx(
+                    out=x0cod[:].bitcast(FP8X4),
+                    scales=x0scl[:],
+                    in_=g0[:].rearrange("p h r b w -> p (h r b w)").bitcast(BF16),
+                )
+                qx1(0)
+            mx_pre(u)
+            qr(u)
+            mx_post(u)
+            fin(u)
+            if u + 1 < NU:
+                tree_b(u + 1)
+                qx1(u + 1)

@@ -22,7 +22,7 @@ RUN = N * C2
 REP = 2
 
 UNITS = (
-    (0, 0, 4, ((0, 2), (2, 4))),
+    (0, 0, 4, ((0, 1, 2), (2, 4))),
     (0, 4, 4, ((4, 8),)),
     (0, 8, 4, ((8, 12),)),
     (0, 12, 4, ((12, 16),)),
@@ -68,6 +68,7 @@ def tile_differentiablelogicmachine_pb_t_kernel(tc, x0, x1, x2, W1, b1, out):
         warm = const.tile([P, 2], F32, name="warm", tag="warm")
         idf = const.tile([P, P], F32, name="idf", tag="idf")
         idb = const.tile([P, P], BF16, name="idb", tag="idb")
+        bbc = const.tile([P, O1], BF16, name="bbc", tag="bbc")
 
         nc.vector.memset(warm[:], 0.0)
         nc.vector.memset(bz[:], 0.0)
@@ -81,9 +82,10 @@ def tile_differentiablelogicmachine_pb_t_kernel(tc, x0, x1, x2, W1, b1, out):
 
         xt = [big.tile([P, N, E, C2], BF16, name="xt%d" % h, tag="xt%d" % h) for h in range(2)]
 
-        def load_x2(u):
+        def load_x2(u, trees=None):
             h = UNITS[u][0]
-            for a, b in UNITS[u][3]:
+            bounds = [p for t in (trees or UNITS[u][3]) for p in zip(t[:-1], t[1:])]
+            for a, b in bounds:
                 g_lo = (E * a + N - 1) // N
                 g_hi = (E * b + N - 1) // N
                 src = x2[h * P:(h + 1) * P].rearrange("b i j c -> b (i j c)")[:, C2:N * N * C2]
@@ -102,16 +104,17 @@ def tile_differentiablelogicmachine_pb_t_kernel(tc, x0, x1, x2, W1, b1, out):
             )
             x1t[u] = t
 
-        load_x2(0)
+        load_x2(0, UNITS[0][3][0:1])
         nc.sync.dma_start(out=wraw[:, S_X1, :, :], in_=W1[C0:C0 + C1, :].rearrange("(p j) o -> p j o", j=4))
         nc.sync.dma_start(out=wraw[:, S_X0, 0:2, :], in_=W1[0:C0, :].rearrange("(p e) o -> p e o", e=2))
         wr_src = W1[C0 + C1:K, :].rearrange("(u p e) o -> p u (e o)", u=2, e=2)
         nc.sync.dma_start(out=wraw[0:64, S_LO, :, :].rearrange("p (u e) o -> p u (e o)", u=2), in_=wr_src)
         nc.sync.dma_start(out=wraw[64:128, S_HI, :, :].rearrange("p (u e) o -> p u (e o)", u=2), in_=wr_src)
+        load_x2(0, UNITS[0][3][1:2])
+        load_x2(1)
         nc.sync.dma_start(out=x0sb[:], in_=x0.rearrange("(h b) k -> b h k", h=2))
         nc.sync.dma_start(out=bz[0:2, :], in_=b1.rearrange("(r c) -> r c", r=2))
         load_x1(0)
-        load_x2(1)
         load_x1(1)
         load_x2(2)
         load_x1(2)
@@ -123,16 +126,17 @@ def tile_differentiablelogicmachine_pb_t_kernel(tc, x0, x1, x2, W1, b1, out):
 
         def level1(u, g):
             h = UNITS[u][0]
-            a, b = UNITS[u][3][g]
+            t = UNITS[u][3][g]
             x = xt[h]
-            m1 = work.tile([P, b - a, 7, C2], BF16, name="m1", tag="m1")
+            m1 = work.tile([P, t[-1] - t[0], 7, C2], BF16, name="m1", tag="m1")
             m1s[(u, g)] = m1
-            tt(out=m1[:], in0=x[:, a:b, 0:7, :], in1=x[:, a:b, 8:15, :], op=ALU.max)
-            tt(out=x[:, a:b, 0:7, :], in0=x[:, a:b, 0:7, :], in1=x[:, a:b, 8:15, :], op=ALU.min)
+            for a, b in zip(t[:-1], t[1:]):
+                tt(out=m1[:, a - t[0]:b - t[0]], in0=x[:, a:b, 0:7, :], in1=x[:, a:b, 8:15, :], op=ALU.max)
+                tt(out=x[:, a:b, 0:7, :], in0=x[:, a:b, 0:7, :], in1=x[:, a:b, 8:15, :], op=ALU.min)
 
         def levels234(u, g):
             h, i0 = UNITS[u][0:2]
-            a, b = UNITS[u][3][g]
+            a, b = UNITS[u][3][g][0], UNITS[u][3][g][-1]
             x = xt[h]
             m1 = m1s[(u, g)]
             rx, rn = rmax[u], rmin[u]
@@ -157,7 +161,11 @@ def tile_differentiablelogicmachine_pb_t_kernel(tc, x0, x1, x2, W1, b1, out):
                 level1(u, g)
                 levels234(u, g)
             nc.vector.tensor_scalar_min(out=rn[:], in0=rn[:], scalar1=1.0)
-            nc.vector.tensor_scalar_max(out=rx[:], in0=rx[:], scalar1=0.0)
+            if u == NU - 1:
+                nc.vector.tensor_scalar_max(out=rx[:], in0=rx[:], scalar1=0.0)
+            else:
+                flat = rx[:].rearrange("p i c -> p (i c)")
+                nc.scalar.activation(out=flat, in_=flat, func=ACTF.Relu)
 
         g1s, x1cs = {}, {}
 
@@ -265,6 +273,43 @@ def tile_differentiablelogicmachine_pb_t_kernel(tc, x0, x1, x2, W1, b1, out):
                     scale=1.0,
                 )
 
+        def last_pass(u, par, kind):
+            h = UNITS[u][0]
+            if kind == 0:
+                slot = S_X1
+                cod, scl = x1cs[u][0][:, par * P:(par + 1) * P], x1cs[u][1][:, par * P:(par + 1) * P]
+            elif kind == 1:
+                slot = S_X0
+                cod, scl = x0cod[:, h * REP * P:h * REP * P + P], x0scl[:, h * REP * P:h * REP * P + P]
+            else:
+                slot = S_LO + par
+                cod, scl = tcs[u][0][:], tcs[u][1][:]
+            cols = slice(slot * O1, (slot + 1) * O1)
+            nc.tensor.matmul_mx(
+                out=accs[(u, par)][:],
+                lhsT=cod.bitcast(FP8X4),
+                lhsT_scale=scl,
+                rhs=wcod[:, cols].bitcast(FP8X4),
+                rhs_scale=wscl[:, cols],
+                start=(kind == 0),
+                stop=(kind == 2),
+            )
+
+        def last_pre(u):
+            for par in range(2):
+                accs[(u, par)] = ps_acc.tile([P, O1], F32, name="acc", tag="acc")
+                last_pass(u, par, 0)
+                last_pass(u, par, 1)
+
+        def last_post(u):
+            h, i0, nr = UNITS[u][0:3]
+            o = work.tile([P, nr, O1], F32, name="osb", tag="osb")
+            for par in range(2):
+                last_pass(u, par, 2)
+                tt(out=o[:, par, :], in0=accs[(u, par)][:], in1=bbc[:], op=ALU.add)
+                nc.scalar.activation(out=o[:, par, :], in_=o[:, par, :], func=ACTF.Sigmoid)
+            nc.sync.dma_start(out=out[h * P:(h + 1) * P, i0:i0 + nr, :], in_=o[:])
+
         def fin(u):
             h, i0, nr = UNITS[u][0:3]
             o = work.tile([P, nr, O1], F32, name="osb", tag="osb")
@@ -304,6 +349,8 @@ def tile_differentiablelogicmachine_pb_t_kernel(tc, x0, x1, x2, W1, b1, out):
                 if u + 6 < NU:
                     load_x2(u + 6)
                     load_x1(u + 6)
+                if u + 6 == NU:
+                    nc.sync.dma_start(out=bbc[:], in_=b1.partition_broadcast(P))
             if u + 1 < NU:
                 tree_a(u + 1)
             if u == 0:
@@ -318,10 +365,17 @@ def tile_differentiablelogicmachine_pb_t_kernel(tc, x0, x1, x2, W1, b1, out):
                     in_=g0[:].rearrange("p h r b w -> p (h r b w)").bitcast(BF16),
                 )
                 qx1(0)
-            mx_pre(u)
+            if u < NU - 1:
+                mx_pre(u)
             qr(u)
-            mx_post(u)
-            fin(u)
+            if u + 1 < NU:
+                qx1(u + 1)
+            if u < NU - 1:
+                mx_post(u)
+                fin(u)
+            else:
+                last_post(u)
+            if u + 1 == NU - 1:
+                last_pre(u + 1)
             if u + 1 < NU:
                 tree_b(u + 1)
-                qx1(u + 1)

@@ -297,7 +297,7 @@ def tile_differentiablelogicmachine_pb_t_kernel(tc, x0, x1, x2, W1, b1, out):
 
         def last_pre(u):
             for par in range(2):
-                accs[(u, par)] = ps_acc.tile([P, O1], F32, name="acc", tag="acc")
+                accs[(u, par)] = ps_tx.tile([P, O1], F32, name="tx", tag="tx")
                 last_pass(u, par, 0)
                 last_pass(u, par, 1)
 
@@ -344,6 +344,8 @@ def tile_differentiablelogicmachine_pb_t_kernel(tc, x0, x1, x2, W1, b1, out):
 
         for u in range(NU):
             tr(u)
+            if u >= 1:
+                fin(u - 1)
             if u + 2 < NU:
                 tx1(u + 2)
                 if u + 6 < NU:
@@ -372,7 +374,6 @@ def tile_differentiablelogicmachine_pb_t_kernel(tc, x0, x1, x2, W1, b1, out):
                 qx1(u + 1)
             if u < NU - 1:
                 mx_post(u)
-                fin(u)
             else:
                 last_post(u)
             if u + 1 == NU - 1:

@@ -69,6 +69,7 @@ def tile_differentiablelogicmachine_pb_t_kernel(tc, x0, x1, x2, W1, b1, out):
         idf = const.tile([P, P], F32, name="idf", tag="idf")
         idb = const.tile([P, P], BF16, name="idb", tag="idb")
         bbc = const.tile([P, O1], BF16, name="bbc", tag="bbc")
+        xtl = const.tile([P, E, P], F32, name="xtl", tag="xtl")
 
         nc.vector.memset(warm[:], 0.0)
         nc.vector.memset(bz[:], 0.0)
@@ -82,7 +83,19 @@ def tile_differentiablelogicmachine_pb_t_kernel(tc, x0, x1, x2, W1, b1, out):
 
         xt = [big.tile([P, N, E, C2], BF16, name="xt%d" % h, tag="xt%d" % h) for h in range(2)]
 
+        xl = xt[1][:, N - 2:N].rearrange("p i e c -> p (i e c)").rearrange("p (e r c) -> p e r c", r=2, c=C2)
+
+        def load_last():
+            for r in range(2):
+                i = N - 2 + r
+                nc.sync.dma_start(out=xl[:, 0:i, r, :], in_=x2[P:2 * P, i, 0:i, :])
+                if i + 1 < N:
+                    nc.sync.dma_start(out=xl[:, i:E, r, :], in_=x2[P:2 * P, i, i + 1:N, :])
+
         def load_x2(u, trees=None):
+            if u == NU - 1:
+                load_last()
+                return
             h = UNITS[u][0]
             bounds = [p for t in (trees or UNITS[u][3]) for p in zip(t[:-1], t[1:])]
             for a, b in bounds:
@@ -121,8 +134,50 @@ def tile_differentiablelogicmachine_pb_t_kernel(tc, x0, x1, x2, W1, b1, out):
         load_x2(3)
         load_x1(3)
 
-        rmax, rmin, m1s = {}, {}, {}
+        rmax, rmin, m1s, gts = {}, {}, {}, {}
         tt = nc.vector.tensor_tensor
+
+        def last_prep():
+            words = xl.rearrange("p e r c -> p e (r c)").bitcast(F32)
+            for e0 in range(0, E, 4):
+                n = min(4, E - e0)
+                bank = ps_tx.tile([P, 4, P], F32, name="tx", tag="tx")
+                for k in range(n):
+                    nc.tensor.transpose(bank[:, k, :], words[:, e0 + k, :], idf[:])
+                nc.scalar.copy(out=xtl[:, e0:e0 + n, :], in_=bank[:, 0:n, :])
+
+        def last_tree_a():
+            x = xtl[:].bitcast(BF16)
+            m1 = work.tile([P, 7, 2 * P], BF16, name="m1", tag="m1")
+            m1s[NU - 1] = m1
+            tt(out=m1[:], in0=x[:, 0:7, :], in1=x[:, 8:15, :], op=ALU.max)
+            tt(out=x[:, 0:7, :], in0=x[:, 0:7, :], in1=x[:, 8:15, :], op=ALU.min)
+
+        def last_tree_b():
+            x = xtl[:].bitcast(BF16)
+            m1 = m1s[NU - 1]
+            gt = work.tile([P, 1, P, 2], F32, name="gt", tag="gt", align_bytes=64)
+            gts[NU - 1] = gt
+            gb = gt[:].rearrange("p r b w -> p (r b w)").bitcast(BF16).rearrange("p (b t) -> p b t", t=4)
+            tt(out=m1[:, 0:3, :], in0=m1[:, 0:3, :], in1=m1[:, 3:6, :], op=ALU.max)
+            tt(out=x[:, 0:4, :], in0=x[:, 0:4, :], in1=x[:, 4:8, :], op=ALU.min)
+            tt(out=m1[:, 3, :], in0=m1[:, 6, :], in1=x[:, 7, :], op=ALU.max)
+            tt(out=x[:, 0:2, :], in0=x[:, 0:2, :], in1=x[:, 2:4, :], op=ALU.min)
+            tt(out=m1[:, 0:2, :], in0=m1[:, 0:2, :], in1=m1[:, 2:4, :], op=ALU.max)
+            nc.vector.tensor_scalar_min(out=x[:, 0, :], in0=x[:, 0, :], scalar1=1.0)
+            nc.vector.tensor_scalar_max(out=m1[:, 0, :], in0=m1[:, 0, :], scalar1=0.0)
+            tt(
+                out=gb[:, :, 2:4],
+                in0=x[:, 0, :].rearrange("p (b e) -> p b e", e=2),
+                in1=x[:, 1, :].rearrange("p (b e) -> p b e", e=2),
+                op=ALU.min,
+            )
+            tt(
+                out=gb[:, :, 0:2],
+                in0=m1[:, 0, :].rearrange("p (b e) -> p b e", e=2),
+                in1=m1[:, 1, :].rearrange("p (b e) -> p b e", e=2),
+                op=ALU.max,
+            )
 
         def level1(u, g):
             h = UNITS[u][0]
@@ -149,9 +204,15 @@ def tile_differentiablelogicmachine_pb_t_kernel(tc, x0, x1, x2, W1, b1, out):
             tt(out=rx[:, a - i0:b - i0, :], in0=m1[:, :, 0, :], in1=m1[:, :, 1, :], op=ALU.max)
 
         def tree_a(u):
-            level1(u, 0)
+            if u == NU - 1:
+                last_tree_a()
+            else:
+                level1(u, 0)
 
         def tree_b(u):
+            if u == NU - 1:
+                last_tree_b()
+                return
             nr = UNITS[u][2]
             rx = work.tile([P, nr, C2], BF16, name="rx", tag="rx")
             rn = work.tile([P, nr, C2], BF16, name="rn", tag="rn")
@@ -161,11 +222,8 @@ def tile_differentiablelogicmachine_pb_t_kernel(tc, x0, x1, x2, W1, b1, out):
                 level1(u, g)
                 levels234(u, g)
             nc.vector.tensor_scalar_min(out=rn[:], in0=rn[:], scalar1=1.0)
-            if u == NU - 1:
-                nc.vector.tensor_scalar_max(out=rx[:], in0=rx[:], scalar1=0.0)
-            else:
-                flat = rx[:].rearrange("p i c -> p (i c)")
-                nc.scalar.activation(out=flat, in_=flat, func=ACTF.Relu)
+            flat = rx[:].rearrange("p i c -> p (i c)")
+            nc.scalar.activation(out=flat, in_=flat, func=ACTF.Relu)
 
         g1s, x1cs = {}, {}
 
@@ -197,7 +255,7 @@ def tile_differentiablelogicmachine_pb_t_kernel(tc, x0, x1, x2, W1, b1, out):
                 in_=g1s[u][:].rearrange("p a r b w -> p (a r b w)").bitcast(BF16),
             )
 
-        gts, tcs = {}, {}
+        tcs = {}
 
         def tr(u):
             npr = UNITS[u][2] // 2
@@ -343,7 +401,8 @@ def tile_differentiablelogicmachine_pb_t_kernel(tc, x0, x1, x2, W1, b1, out):
             load_x1(u + 4)
 
         for u in range(NU):
-            tr(u)
+            if u < NU - 1:
+                tr(u)
             if u >= 1:
                 fin(u - 1)
             if u + 2 < NU:
@@ -353,6 +412,8 @@ def tile_differentiablelogicmachine_pb_t_kernel(tc, x0, x1, x2, W1, b1, out):
                     load_x1(u + 6)
                 if u + 6 == NU:
                     nc.sync.dma_start(out=bbc[:], in_=b1.partition_broadcast(P))
+                if u + 5 == NU:
+                    last_prep()
             if u + 1 < NU:
                 tree_a(u + 1)
             if u == 0:

@@ -34,6 +34,8 @@ UNITS = (
 )
 NU = 9
 assert len(UNITS) == NU
+XR = 4
+NX = (B // P) * (N // XR)
 
 FLOPS = 2 * B * N * K * O1
 BYTES = 2 * (B * C0 + B * N * C1 + B * N * E * C2 + K * O1 + O1) + 4 * B * N * O1
@@ -69,7 +71,6 @@ def tile_differentiablelogicmachine_pb_t_kernel(tc, x0, x1, x2, W1, b1, out):
         idf = const.tile([P, P], F32, name="idf", tag="idf")
         idb = const.tile([P, P], BF16, name="idb", tag="idb")
         bbc = const.tile([P, O1], BF16, name="bbc", tag="bbc")
-        xtl = const.tile([P, E, P], F32, name="xtl", tag="xtl")
 
         nc.vector.memset(warm[:], 0.0)
         nc.vector.memset(bz[:], 0.0)
@@ -83,19 +84,7 @@ def tile_differentiablelogicmachine_pb_t_kernel(tc, x0, x1, x2, W1, b1, out):
 
         xt = [big.tile([P, N, E, C2], BF16, name="xt%d" % h, tag="xt%d" % h) for h in range(2)]
 
-        xl = xt[1][:, N - 2:N].rearrange("p i e c -> p (i e c)").rearrange("p (e r c) -> p e r c", r=2, c=C2)
-
-        def load_last():
-            for r in range(2):
-                i = N - 2 + r
-                nc.sync.dma_start(out=xl[:, 0:i, r, :], in_=x2[P:2 * P, i, 0:i, :])
-                if i + 1 < N:
-                    nc.sync.dma_start(out=xl[:, i:E, r, :], in_=x2[P:2 * P, i, i + 1:N, :])
-
         def load_x2(u, trees=None):
-            if u == NU - 1:
-                load_last()
-                return
             h = UNITS[u][0]
             bounds = [p for t in (trees or UNITS[u][3]) for p in zip(t[:-1], t[1:])]
             for a, b in bounds:
@@ -108,14 +97,14 @@ def tile_differentiablelogicmachine_pb_t_kernel(tc, x0, x1, x2, W1, b1, out):
 
         x1t = {}
 
-        def load_x1(u):
-            h, i0, nr = UNITS[u][0:3]
-            t = x1p.tile([P, nr * C1], BF16, name="x1t", tag="x1t")
+        def load_x1(v):
+            h, q = divmod(v, N // XR)
+            t = x1p.tile([P, XR * C1], BF16, name="x1t", tag="x1t")
             nc.sync.dma_start(
                 out=t[:].rearrange("p (i k) -> p i k", k=C1),
-                in_=x1[h * P:(h + 1) * P, i0:i0 + nr, :],
+                in_=x1[h * P:(h + 1) * P, q * XR:(q + 1) * XR, :],
             )
-            x1t[u] = t
+            x1t[v] = t
 
         load_x2(0, UNITS[0][3][0:1])
         nc.sync.dma_start(out=wraw[:, S_X1, :, :], in_=W1[C0:C0 + C1, :].rearrange("(p j) o -> p j o", j=4))
@@ -134,50 +123,8 @@ def tile_differentiablelogicmachine_pb_t_kernel(tc, x0, x1, x2, W1, b1, out):
         load_x2(3)
         load_x1(3)
 
-        rmax, rmin, m1s, gts = {}, {}, {}, {}
+        rmax, rmin, m1s = {}, {}, {}
         tt = nc.vector.tensor_tensor
-
-        def last_prep():
-            words = xl.rearrange("p e r c -> p e (r c)").bitcast(F32)
-            for e0 in range(0, E, 4):
-                n = min(4, E - e0)
-                bank = ps_tx.tile([P, 4, P], F32, name="tx", tag="tx")
-                for k in range(n):
-                    nc.tensor.transpose(bank[:, k, :], words[:, e0 + k, :], idf[:])
-                nc.scalar.copy(out=xtl[:, e0:e0 + n, :], in_=bank[:, 0:n, :])
-
-        def last_tree_a():
-            x = xtl[:].bitcast(BF16)
-            m1 = work.tile([P, 7, 2 * P], BF16, name="m1", tag="m1")
-            m1s[NU - 1] = m1
-            tt(out=m1[:], in0=x[:, 0:7, :], in1=x[:, 8:15, :], op=ALU.max)
-            tt(out=x[:, 0:7, :], in0=x[:, 0:7, :], in1=x[:, 8:15, :], op=ALU.min)
-
-        def last_tree_b():
-            x = xtl[:].bitcast(BF16)
-            m1 = m1s[NU - 1]
-            gt = work.tile([P, 1, P, 2], F32, name="gt", tag="gt", align_bytes=64)
-            gts[NU - 1] = gt
-            gb = gt[:].rearrange("p r b w -> p (r b w)").bitcast(BF16).rearrange("p (b t) -> p b t", t=4)
-            tt(out=m1[:, 0:3, :], in0=m1[:, 0:3, :], in1=m1[:, 3:6, :], op=ALU.max)
-            tt(out=x[:, 0:4, :], in0=x[:, 0:4, :], in1=x[:, 4:8, :], op=ALU.min)
-            tt(out=m1[:, 3, :], in0=m1[:, 6, :], in1=x[:, 7, :], op=ALU.max)
-            tt(out=x[:, 0:2, :], in0=x[:, 0:2, :], in1=x[:, 2:4, :], op=ALU.min)
-            tt(out=m1[:, 0:2, :], in0=m1[:, 0:2, :], in1=m1[:, 2:4, :], op=ALU.max)
-            nc.vector.tensor_scalar_min(out=x[:, 0, :], in0=x[:, 0, :], scalar1=1.0)
-            nc.vector.tensor_scalar_max(out=m1[:, 0, :], in0=m1[:, 0, :], scalar1=0.0)
-            tt(
-                out=gb[:, :, 2:4],
-                in0=x[:, 0, :].rearrange("p (b e) -> p b e", e=2),
-                in1=x[:, 1, :].rearrange("p (b e) -> p b e", e=2),
-                op=ALU.min,
-            )
-            tt(
-                out=gb[:, :, 0:2],
-                in0=m1[:, 0, :].rearrange("p (b e) -> p b e", e=2),
-                in1=m1[:, 1, :].rearrange("p (b e) -> p b e", e=2),
-                op=ALU.max,
-            )
 
         def level1(u, g):
             h = UNITS[u][0]
@@ -204,15 +151,9 @@ def tile_differentiablelogicmachine_pb_t_kernel(tc, x0, x1, x2, W1, b1, out):
             tt(out=rx[:, a - i0:b - i0, :], in0=m1[:, :, 0, :], in1=m1[:, :, 1, :], op=ALU.max)
 
         def tree_a(u):
-            if u == NU - 1:
-                last_tree_a()
-            else:
-                level1(u, 0)
+            level1(u, 0)
 
         def tree_b(u):
-            if u == NU - 1:
-                last_tree_b()
-                return
             nr = UNITS[u][2]
             rx = work.tile([P, nr, C2], BF16, name="rx", tag="rx")
             rn = work.tile([P, nr, C2], BF16, name="rn", tag="rn")
@@ -222,13 +163,16 @@ def tile_differentiablelogicmachine_pb_t_kernel(tc, x0, x1, x2, W1, b1, out):
                 level1(u, g)
                 levels234(u, g)
             nc.vector.tensor_scalar_min(out=rn[:], in0=rn[:], scalar1=1.0)
-            flat = rx[:].rearrange("p i c -> p (i c)")
-            nc.scalar.activation(out=flat, in_=flat, func=ACTF.Relu)
+            if u == NU - 1:
+                nc.vector.tensor_scalar_max(out=rx[:], in0=rx[:], scalar1=0.0)
+            else:
+                flat = rx[:].rearrange("p i c -> p (i c)")
+                nc.scalar.activation(out=flat, in_=flat, func=ACTF.Relu)
 
         g1s, x1cs = {}, {}
 
         def tx1(u):
-            npr = UNITS[u][2] // 2
+            npr = XR // 2
             words = x1t[u][:].bitcast(F32)
             g1 = work.tile([P, 2, npr, P, 2], F32, name="g1", tag="g1", align_bytes=64)
             g1s[u] = g1
@@ -245,7 +189,7 @@ def tile_differentiablelogicmachine_pb_t_kernel(tc, x0, x1, x2, W1, b1, out):
                 nc.scalar.copy(out=g1[:, par], in_=bank[:].rearrange("p r w b -> p r b w"))
 
         def qx1(u):
-            ncol = UNITS[u][2] // 2 * P
+            ncol = XR // 2 * P
             cod = work.tile([P, 2 * ncol], U32, name="x1cod", tag="x1cod", align_bytes=64)
             scl = work.tile([P, 2 * ncol], U8, name="x1scl", tag="x1scl", align_bytes=64)
             x1cs[u] = (cod, scl)
@@ -255,7 +199,7 @@ def tile_differentiablelogicmachine_pb_t_kernel(tc, x0, x1, x2, W1, b1, out):
                 in_=g1s[u][:].rearrange("p a r b w -> p (a r b w)").bitcast(BF16),
             )
 
-        tcs = {}
+        gts, tcs = {}, {}
 
         def tr(u):
             npr = UNITS[u][2] // 2
@@ -282,13 +226,18 @@ def tile_differentiablelogicmachine_pb_t_kernel(tc, x0, x1, x2, W1, b1, out):
 
         sig, accs = {}, {}
 
+        def x1_cols(u, par):
+            h, i0 = UNITS[u][0:2]
+            return h * (N // XR) + i0 // XR, (par * (XR // 2) + (i0 % XR) // 2) * P
+
         def mx_pass(u, oh, par, kind):
             h = UNITS[u][0]
             ncol = UNITS[u][2] // 2 * P
             if kind == 0:
                 slot = S_X1
-                cod = x1cs[u][0][:, par * ncol:(par + 1) * ncol]
-                scl = x1cs[u][1][:, par * ncol:(par + 1) * ncol]
+                v, lo = x1_cols(u, par)
+                cod = x1cs[v][0][:, lo:lo + ncol]
+                scl = x1cs[v][1][:, lo:lo + ncol]
             elif kind == 1:
                 slot = S_X0
                 cod = x0cod[:, h * REP * P:h * REP * P + ncol]
@@ -335,7 +284,8 @@ def tile_differentiablelogicmachine_pb_t_kernel(tc, x0, x1, x2, W1, b1, out):
             h = UNITS[u][0]
             if kind == 0:
                 slot = S_X1
-                cod, scl = x1cs[u][0][:, par * P:(par + 1) * P], x1cs[u][1][:, par * P:(par + 1) * P]
+                v, lo = x1_cols(u, par)
+                cod, scl = x1cs[v][0][:, lo:lo + P], x1cs[v][1][:, lo:lo + P]
             elif kind == 1:
                 slot = S_X0
                 cod, scl = x0cod[:, h * REP * P:h * REP * P + P], x0scl[:, h * REP * P:h * REP * P + P]
@@ -401,19 +351,17 @@ def tile_differentiablelogicmachine_pb_t_kernel(tc, x0, x1, x2, W1, b1, out):
             load_x1(u + 4)
 
         for u in range(NU):
-            if u < NU - 1:
-                tr(u)
+            tr(u)
             if u >= 1:
                 fin(u - 1)
-            if u + 2 < NU:
+            if u + 2 < NX:
                 tx1(u + 2)
-                if u + 6 < NU:
-                    load_x2(u + 6)
-                    load_x1(u + 6)
-                if u + 6 == NU:
-                    nc.sync.dma_start(out=bbc[:], in_=b1.partition_broadcast(P))
-                if u + 5 == NU:
-                    last_prep()
+            if u + 6 < NU:
+                load_x2(u + 6)
+            if u + 6 < NX:
+                load_x1(u + 6)
+            if u + 6 == NU:
+                nc.sync.dma_start(out=bbc[:], in_=b1.partition_broadcast(P))
             if u + 1 < NU:
                 tree_a(u + 1)
             if u == 0:
@@ -431,7 +379,7 @@ def tile_differentiablelogicmachine_pb_t_kernel(tc, x0, x1, x2, W1, b1, out):
             if u < NU - 1:
                 mx_pre(u)
             qr(u)
-            if u + 1 < NU:
+            if u + 1 < NX:
                 qx1(u + 1)
             if u < NU - 1:
                 mx_post(u)

@@ -23,7 +23,7 @@ REP = 2
 
 UNITS = (
     (0, 0, 4, ((0, 1, 2), (2, 4))),
-    (0, 4, 4, ((4, 8),)),
+    (0, 4, 4, ((4, 6, 8),)),
     (0, 8, 4, ((8, 12),)),
     (0, 12, 4, ((12, 16),)),
     (1, 0, 4, ((0, 4),)),
@@ -50,9 +50,9 @@ def tile_differentiablelogicmachine_pb_t_kernel(tc, x0, x1, x2, W1, b1, out):
         big = ctx.enter_context(tc.tile_pool(name="big", bufs=1))
         x1p = ctx.enter_context(tc.tile_pool(name="x1p", bufs=4))
         work = ctx.enter_context(tc.tile_pool(name="work", bufs=2))
-        ps_init = ctx.enter_context(tc.psum_pool(name="ps_init", bufs=1))
+        outp = ctx.enter_context(tc.tile_pool(name="outp", bufs=3))
         ps_tx = ctx.enter_context(tc.psum_pool(name="ps_tx", bufs=2))
-        ps_tr = ctx.enter_context(tc.psum_pool(name="ps_tr", bufs=1))
+        ps_tr = ctx.enter_context(tc.psum_pool(name="ps_tr", bufs=2))
         ps_acc = ctx.enter_context(tc.psum_pool(name="ps_acc", bufs=2))
         ps_ot = ctx.enter_context(tc.psum_pool(name="ps_ot", bufs=2))
         ctx.enter_context(tc.manual_schedule())
@@ -74,9 +74,9 @@ def tile_differentiablelogicmachine_pb_t_kernel(tc, x0, x1, x2, W1, b1, out):
 
         nc.vector.memset(warm[:], 0.0)
         nc.vector.memset(bz[:], 0.0)
-        nc.vector.memset(wraw[:, S_X0, 2:4, :], 0.0)
-        nc.vector.memset(wraw[64:128, S_LO, :, :], 0.0)
-        nc.vector.memset(wraw[0:64, S_HI, :, :], 0.0)
+        nc.gpsimd.memset(wraw[:, S_X0, 2:4, :], 0.0)
+        nc.gpsimd.memset(wraw[64:128, S_LO, :, :], 0.0)
+        nc.gpsimd.memset(wraw[0:64, S_HI, :, :], 0.0)
         nc.vector.memset(g0[:], 0.0)
         make_identity(nc, idf[:])
         make_identity(nc, idb[:])
@@ -84,10 +84,10 @@ def tile_differentiablelogicmachine_pb_t_kernel(tc, x0, x1, x2, W1, b1, out):
 
         xt = [big.tile([P, N, E, C2], BF16, name="xt%d" % h, tag="xt%d" % h) for h in range(2)]
 
-        def load_x2(u, trees=None):
+        def load_x2(u, steps=slice(0, 3)):
             h = UNITS[u][0]
-            bounds = [p for t in (trees or UNITS[u][3]) for p in zip(t[:-1], t[1:])]
-            for a, b in bounds:
+            bounds = [p for t in UNITS[u][3] for p in zip(t[:-1], t[1:])]
+            for a, b in bounds[steps]:
                 g_lo = (E * a + N - 1) // N
                 g_hi = (E * b + N - 1) // N
                 src = x2[h * P:(h + 1) * P].rearrange("b i j c -> b (i j c)")[:, C2:N * N * C2]
@@ -106,14 +106,14 @@ def tile_differentiablelogicmachine_pb_t_kernel(tc, x0, x1, x2, W1, b1, out):
             )
             x1t[v] = t
 
-        load_x2(0, UNITS[0][3][0:1])
+        load_x2(0)
+        load_x2(1, slice(0, 1))
         nc.sync.dma_start(out=wraw[:, S_X1, :, :], in_=W1[C0:C0 + C1, :].rearrange("(p j) o -> p j o", j=4))
         nc.sync.dma_start(out=wraw[:, S_X0, 0:2, :], in_=W1[0:C0, :].rearrange("(p e) o -> p e o", e=2))
         wr_src = W1[C0 + C1:K, :].rearrange("(u p e) o -> p u (e o)", u=2, e=2)
         nc.sync.dma_start(out=wraw[0:64, S_LO, :, :].rearrange("p (u e) o -> p u (e o)", u=2), in_=wr_src)
         nc.sync.dma_start(out=wraw[64:128, S_HI, :, :].rearrange("p (u e) o -> p u (e o)", u=2), in_=wr_src)
-        load_x2(0, UNITS[0][3][1:2])
-        load_x2(1)
+        load_x2(1, slice(1, 2))
         nc.sync.dma_start(out=x0sb[:], in_=x0.rearrange("(h b) k -> b h k", h=2))
         nc.sync.dma_start(out=bz[0:2, :], in_=b1.rearrange("(r c) -> r c", r=2))
         load_x1(0)
@@ -126,48 +126,73 @@ def tile_differentiablelogicmachine_pb_t_kernel(tc, x0, x1, x2, W1, b1, out):
         rmax, rmin, m1s = {}, {}, {}
         tt = nc.vector.tensor_tensor
 
-        def level1(u, g):
-            h = UNITS[u][0]
-            t = UNITS[u][3][g]
-            x = xt[h]
-            m1 = work.tile([P, t[-1] - t[0], 7, C2], BF16, name="m1", tag="m1")
-            m1s[(u, g)] = m1
-            for a, b in zip(t[:-1], t[1:]):
-                tt(out=m1[:, a - t[0]:b - t[0]], in0=x[:, a:b, 0:7, :], in1=x[:, a:b, 8:15, :], op=ALU.max)
-                tt(out=x[:, a:b, 0:7, :], in0=x[:, a:b, 0:7, :], in1=x[:, a:b, 8:15, :], op=ALU.min)
+        def rows(u, k):
+            t = UNITS[u][3][k]
+            return xt[UNITS[u][0]], t[0], t[-1], UNITS[u][1]
 
-        def levels234(u, g):
-            h, i0 = UNITS[u][0:2]
-            a, b = UNITS[u][3][g][0], UNITS[u][3][g][-1]
-            x = xt[h]
-            m1 = m1s[(u, g)]
-            rx, rn = rmax[u], rmin[u]
+        def a1(u, k, a, b):
+            x, lo, hi, i0 = rows(u, k)
+            if a == lo:
+                m1s[(u, k)] = work.tile([P, hi - lo, 7, C2], BF16, name="m1", tag="m1")
+            m1 = m1s[(u, k)]
+            tt(out=m1[:, a - lo:b - lo], in0=x[:, a:b, 0:7, :], in1=x[:, a:b, 8:15, :], op=ALU.max)
+
+        def a2(u, a, b):
+            x = xt[UNITS[u][0]]
+            tt(out=x[:, a:b, 0:7, :], in0=x[:, a:b, 0:7, :], in1=x[:, a:b, 8:15, :], op=ALU.min)
+
+        def level1(u):
+            a, b = UNITS[u][1], UNITS[u][1] + UNITS[u][2]
+            m = (a + b) // 2
+            a1(u, 0, a, m)
+            a1(u, 0, m, b)
+            a2(u, a, m)
+            a2(u, m, b)
+
+        def c(u, k=0):
+            x, a, b, i0 = rows(u, k)
+            m1 = m1s[(u, k)]
+            tt(out=m1[:, :, 6, :], in0=m1[:, :, 6, :], in1=x[:, a:b, 7, :], op=ALU.max)
+
+        def bb1(u, k=0):
+            m1 = m1s[(u, k)]
             tt(out=m1[:, :, 0:3, :], in0=m1[:, :, 0:3, :], in1=m1[:, :, 3:6, :], op=ALU.max)
+
+        def zn(u, k=0):
+            x, a, b, i0 = rows(u, k)
+            nc.vector.tensor_scalar_min(out=x[:, a:b, 7, :], in0=x[:, a:b, 7, :], scalar1=1.0)
+
+        def zx(u, k=0):
+            m1 = m1s[(u, k)]
+            nc.vector.tensor_scalar_max(out=m1[:, :, 6, :], in0=m1[:, :, 6, :], scalar1=0.0)
+
+        def bb2(u, k=0):
+            x, a, b, i0 = rows(u, k)
             tt(out=x[:, a:b, 0:4, :], in0=x[:, a:b, 0:4, :], in1=x[:, a:b, 4:8, :], op=ALU.min)
-            tt(out=m1[:, :, 3, :], in0=m1[:, :, 6, :], in1=x[:, a:b, 7, :], op=ALU.max)
+
+        def d1(u, k=0):
+            m1 = m1s[(u, k)]
+            tt(out=m1[:, :, 0:2, :], in0=m1[:, :, 0:2, :], in1=m1[:, :, 2:7:4, :], op=ALU.max)
+
+        def d2(u, k=0):
+            x, a, b, i0 = rows(u, k)
             tt(out=x[:, a:b, 0:2, :], in0=x[:, a:b, 0:2, :], in1=x[:, a:b, 2:4, :], op=ALU.min)
-            tt(out=m1[:, :, 0:2, :], in0=m1[:, :, 0:2, :], in1=m1[:, :, 2:4, :], op=ALU.max)
-            tt(out=rn[:, a - i0:b - i0, :], in0=x[:, a:b, 0, :], in1=x[:, a:b, 1, :], op=ALU.min)
-            tt(out=rx[:, a - i0:b - i0, :], in0=m1[:, :, 0, :], in1=m1[:, :, 1, :], op=ALU.max)
 
-        def tree_a(u):
-            level1(u, 0)
+        def e1(u, k=0):
+            x, a, b, i0 = rows(u, k)
+            if k == 0:
+                rmax[u] = work.tile([P, UNITS[u][2], C2], BF16, name="rx", tag="rx")
+                rmin[u] = work.tile([P, UNITS[u][2], C2], BF16, name="rn", tag="rn")
+            m1 = m1s[(u, k)]
+            tt(out=rmax[u][:, a - i0:b - i0, :], in0=m1[:, :, 0, :], in1=m1[:, :, 1, :], op=ALU.max)
 
-        def tree_b(u):
-            nr = UNITS[u][2]
-            rx = work.tile([P, nr, C2], BF16, name="rx", tag="rx")
-            rn = work.tile([P, nr, C2], BF16, name="rn", tag="rn")
-            rmax[u], rmin[u] = rx, rn
-            levels234(u, 0)
-            for g in range(1, len(UNITS[u][3])):
-                level1(u, g)
-                levels234(u, g)
-            nc.vector.tensor_scalar_min(out=rn[:], in0=rn[:], scalar1=1.0)
-            if u == NU - 1:
-                nc.vector.tensor_scalar_max(out=rx[:], in0=rx[:], scalar1=0.0)
-            else:
-                flat = rx[:].rearrange("p i c -> p (i c)")
-                nc.scalar.activation(out=flat, in_=flat, func=ACTF.Relu)
+        def e2(u, k=0):
+            x, a, b, i0 = rows(u, k)
+            tt(out=rmin[u][:, a - i0:b - i0, :], in0=x[:, a:b, 0, :], in1=x[:, a:b, 1, :], op=ALU.min)
+
+        def relu(u):
+            flat = rmax[u][:].rearrange("p i c -> p (i c)")
+            nc.scalar.activation(out=flat, in_=flat, func=ACTF.Relu)
 
         g1s, x1cs = {}, {}
 
@@ -257,19 +282,15 @@ def tile_differentiablelogicmachine_pb_t_kernel(tc, x0, x1, x2, W1, b1, out):
                 stop=(kind == 2),
             )
 
-        def mx_pre(u):
-            ncol = UNITS[u][2] // 2 * P
-            for oh in range(2):
-                accs[(u, oh)] = ps_acc.tile([P, 2, ncol], F32, name="acc", tag="acc")
-                mx_pass(u, oh, 0, 0)
-                mx_pass(u, oh, 0, 1)
-
-        def mx_post(u):
+        def mx(u):
             npr = UNITS[u][2] // 2
             for oh in range(2):
-                mx_pass(u, oh, 0, 2)
+                accs[(u, oh)] = ps_acc.tile([P, 2, npr * P], F32, name="acc", tag="acc")
+            for par in range(2):
                 for kind in range(3):
-                    mx_pass(u, oh, 1, kind)
+                    for oh in range(2):
+                        mx_pass(u, oh, par, kind)
+            for oh in range(2):
                 s = work.tile([P, 2, npr, P], F32, name="sig%d" % oh, tag="sig%d" % oh)
                 sig[(u, oh)] = s
                 nc.scalar.activation(
@@ -280,7 +301,7 @@ def tile_differentiablelogicmachine_pb_t_kernel(tc, x0, x1, x2, W1, b1, out):
                     scale=1.0,
                 )
 
-        def last_pass(u, par, kind):
+        def last_pass(u, par, kind, start=False, stop=False):
             h = UNITS[u][0]
             if kind == 0:
                 slot = S_X1
@@ -299,28 +320,31 @@ def tile_differentiablelogicmachine_pb_t_kernel(tc, x0, x1, x2, W1, b1, out):
                 lhsT_scale=scl,
                 rhs=wcod[:, cols].bitcast(FP8X4),
                 rhs_scale=wscl[:, cols],
-                start=(kind == 0),
-                stop=(kind == 2),
+                start=start,
+                stop=stop,
             )
 
-        def last_pre(u):
-            for par in range(2):
-                accs[(u, par)] = ps_tx.tile([P, O1], F32, name="tx", tag="tx")
-                last_pass(u, par, 0)
-                last_pass(u, par, 1)
+        osbs = {}
 
-        def last_post(u):
-            h, i0, nr = UNITS[u][0:3]
-            o = work.tile([P, nr, O1], F32, name="osb", tag="osb")
+        def last_open(u, pool, tag):
+            nr = UNITS[u][2]
+            osbs[u] = work.tile([P, nr, O1], F32, name="olast", tag="olast")
             for par in range(2):
-                last_pass(u, par, 2)
-                tt(out=o[:, par, :], in0=accs[(u, par)][:], in1=bbc[:], op=ALU.add)
-                nc.scalar.activation(out=o[:, par, :], in_=o[:, par, :], func=ACTF.Sigmoid)
-            nc.sync.dma_start(out=out[h * P:(h + 1) * P, i0:i0 + nr, :], in_=o[:])
+                accs[(u, par)] = pool.tile([P, O1], F32, name=tag, tag=tag)
+                last_pass(u, par, 1, start=True)
+
+        def last_out(u, par):
+            o = osbs[u]
+            tt(out=o[:, par, :], in0=accs[(u, par)][:], in1=bbc[:], op=ALU.add)
+            nc.scalar.activation(out=o[:, par, :], in_=o[:, par, :], func=ACTF.Sigmoid)
+
+        def last_store(u):
+            h, i0, nr = UNITS[u][0:3]
+            nc.sync.dma_start(out=out[h * P:(h + 1) * P, i0:i0 + nr, :], in_=osbs[u][:])
 
         def fin(u):
             h, i0, nr = UNITS[u][0:3]
-            o = work.tile([P, nr, O1], F32, name="osb", tag="osb")
+            o = outp.tile([P, nr, O1], F32, name="osb", tag="osb")
             for pr in range(nr // 2):
                 bank = ps_ot.tile([P, 2, 2, P], F32, name="ot", tag="ot")
                 for par in range(2):
@@ -334,26 +358,21 @@ def tile_differentiablelogicmachine_pb_t_kernel(tc, x0, x1, x2, W1, b1, out):
 
         for s in range(4):
             nc.scalar.copy(out=wgrp[:, s], in_=wraw[:, s].rearrange("p j o -> p o j"))
-        pb = ps_tr.tile([P, P], BF16, name="pb", tag="trb")
+        pb = ps_ot.tile([P, P], BF16, name="pb", tag="ot")
         nc.tensor.transpose(pb[:], bz[:], idb[:])
         nc.scalar.copy(out=bias[:], in_=pb[:, 0:2])
-        p0 = ps_init.tile([P, 2, P], F32, name="p0", tag="init")
+        p0 = ps_ot.tile([P, 2, P], F32, name="p0", tag="ot")
         for h in range(2):
             nc.tensor.transpose(p0[:, h, :], x0sb[:, h, :].bitcast(F32), idf[:])
         for rep in range(REP):
             nc.scalar.copy(out=g0[:, :, rep, :, 0], in_=p0[:])
 
-        tree_a(0)
-        tree_b(0)
         for u in range(2):
             tx1(u)
             load_x2(u + 4)
             load_x1(u + 4)
 
-        for u in range(NU):
-            tr(u)
-            if u >= 1:
-                fin(u - 1)
+        def ahead(u):
             if u + 2 < NX:
                 tx1(u + 2)
             if u + 6 < NU:
@@ -362,30 +381,129 @@ def tile_differentiablelogicmachine_pb_t_kernel(tc, x0, x1, x2, W1, b1, out):
                 load_x1(u + 6)
             if u + 6 == NU:
                 nc.sync.dma_start(out=bbc[:], in_=b1.partition_broadcast(P))
-            if u + 1 < NU:
-                tree_a(u + 1)
-            if u == 0:
-                nc.vector.quantize_mx(
-                    out=wcod[:].bitcast(FP8X4),
-                    scales=wscl[:],
-                    in_=wgrp[:].rearrange("p s o j -> p (s o j)"),
-                )
-                nc.vector.quantize_mx(
-                    out=x0cod[:].bitcast(FP8X4),
-                    scales=x0scl[:],
-                    in_=g0[:].rearrange("p h r b w -> p (h r b w)").bitcast(BF16),
-                )
-                qx1(0)
-            if u < NU - 1:
-                mx_pre(u)
+
+        def quantize_w():
+            nc.vector.quantize_mx(
+                out=wcod[:].bitcast(FP8X4),
+                scales=wscl[:],
+                in_=wgrp[:].rearrange("p s o j -> p (s o j)"),
+            )
+
+        def quantize_x0():
+            nc.vector.quantize_mx(
+                out=x0cod[:].bitcast(FP8X4),
+                scales=x0scl[:],
+                in_=g0[:].rearrange("p h r b w -> p (h r b w)").bitcast(BF16),
+            )
+
+        a1(0, 0, 0, 1)
+        a1(0, 0, 1, 2)
+        a2(0, 0, 1)
+        a2(0, 1, 2)
+        c(0, 0)
+        bb1(0, 0)
+        zn(0, 0)
+        zx(0, 0)
+        a1(0, 1, 2, 4)
+        bb2(0, 0)
+        d1(0, 0)
+        a2(0, 2, 4)
+        d2(0, 0)
+        c(0, 1)
+        e1(0, 0)
+        bb1(0, 1)
+        e2(0, 0)
+        zn(0, 1)
+        zx(0, 1)
+        a1(1, 0, 4, 6)
+        bb2(0, 1)
+        d1(0, 1)
+        a2(1, 4, 6)
+        d2(0, 1)
+        e1(0, 1)
+        a1(1, 0, 6, 8)
+        e2(0, 1)
+        quantize_w()
+        a2(1, 6, 8)
+        tr(0)
+        ahead(0)
+        quantize_x0()
+        c(1)
+        bb1(1)
+        zn(1)
+        qx1(0)
+        bb2(1)
+        qr(0)
+        d1(1)
+        d2(1)
+        qx1(1)
+        e1(1)
+        e2(1)
+        mx(0)
+
+        for u in range(1, NU - 3):
+            level1(u + 1)
+            relu(u)
+            tr(u)
+            fin(u - 1)
+            ahead(u)
+            c(u + 1)
+            bb1(u + 1)
+            zn(u + 1)
             qr(u)
-            if u + 1 < NX:
+            bb2(u + 1)
+            d1(u + 1)
+            d2(u + 1)
+            if u + 1 < NX - 1:
                 qx1(u + 1)
-            if u < NU - 1:
-                mx_post(u)
-            else:
-                last_post(u)
-            if u + 1 == NU - 1:
-                last_pre(u + 1)
-            if u + 1 < NU:
-                tree_b(u + 1)
+            e1(u + 1)
+            e2(u + 1)
+            mx(u)
+
+        uz, ua, ub = NU - 3, NU - 2, NU - 1
+        level1(ua)
+        relu(uz)
+        tr(uz)
+        fin(uz - 1)
+        c(ua)
+        bb1(ua)
+        zn(ua)
+        zx(ua)
+        a1(ub, 0, 14, 16)
+        bb2(ua)
+        d1(ua)
+        qr(uz)
+        d2(ua)
+        a2(ub, 14, 16)
+        mx(uz)
+        e1(ua)
+        c(ub)
+        e2(ua)
+        tr(ua)
+        bb1(ub)
+        zn(ub)
+        zx(ub)
+        bb2(ub)
+        d1(ub)
+        d2(ub)
+        e1(ub)
+        e2(ub)
+        last_open(ub, ps_tx, "tx")
+        fin(uz)
+        last_open(ua, ps_acc, "acc")
+        tr(ub)
+        qr(ua)
+        qx1(ua)
+        for par in range(2):
+            last_pass(ua, par, 2)
+        for par in range(2):
+            last_pass(ua, par, 0, stop=True)
+        for par in range(2):
+            last_pass(ub, par, 0)
+        qr(ub)
+        for par in range(2):
+            last_pass(ub, par, 2, stop=True)
+        for u in (ua, ub):
+            for par in range(2):
+                last_out(u, par)
+            last_store(u)

@@ -19,10 +19,9 @@ B, N, C0, C1, C2, O1 = 256, 16, 256, 512, 128, 256
 K = C0 + C1 + 2 * C2
 E = N - 1
 RUN = N * C2
-REP = 2
 
 UNITS = (
-    (0, 0, 4, ((0, 1, 2), (2, 4))),
+    (0, 0, 4, ((0, 1), (1, 2), (2, 4))),
     (0, 4, 4, ((4, 6, 8),)),
     (0, 8, 4, ((8, 12),)),
     (0, 12, 4, ((12, 16),)),
@@ -62,9 +61,9 @@ def tile_differentiablelogicmachine_pb_t_kernel(tc, x0, x1, x2, W1, b1, out):
         wcod = const.tile([P, 4 * O1], U32, name="wcod", tag="wcod", align_bytes=64)
         wscl = const.tile([P, 4 * O1], U8, name="wscl", tag="wscl", align_bytes=64)
         x0sb = const.tile([P, 2, C0], BF16, name="x0sb", tag="x0sb")
-        g0 = const.tile([P, 2, REP, P, 2], F32, name="g0", tag="g0", align_bytes=64)
-        x0cod = const.tile([P, 2 * REP * P], U32, name="x0cod", tag="x0cod", align_bytes=64)
-        x0scl = const.tile([P, 2 * REP * P], U8, name="x0scl", tag="x0scl", align_bytes=64)
+        g0 = const.tile([P, 2, P, 2], F32, name="g0", tag="g0", align_bytes=64)
+        x0cod = const.tile([P, 2 * P], U32, name="x0cod", tag="x0cod", align_bytes=64)
+        x0scl = const.tile([P, 2 * P], U8, name="x0scl", tag="x0scl", align_bytes=64)
         bz = const.tile([P, P], BF16, name="bz", tag="bz")
         bias = const.tile([P, 2], F32, name="bias", tag="bias")
         warm = const.tile([P, 2], F32, name="warm", tag="warm")
@@ -106,7 +105,11 @@ def tile_differentiablelogicmachine_pb_t_kernel(tc, x0, x1, x2, W1, b1, out):
             )
             x1t[v] = t
 
-        load_x2(0)
+        first = x2[0:P].rearrange("b i j c -> b (i j c)")[:, C2:C2 + RUN].rearrange("b (s e c) -> b s (e c)", s=2, c=C2)
+        row0 = xt[0][:].rearrange("p i e c -> p (i e c)")[:, 0:RUN].rearrange("p (s f) -> p s f", s=2)
+        for lo, hi in ((0, 4), (4, 8)):
+            nc.sync.dma_start(out=row0[:, :, lo * C2:hi * C2], in_=first[:, :, lo * C2:hi * C2])
+        load_x2(0, slice(1, 3))
         load_x2(1, slice(0, 1))
         nc.sync.dma_start(out=wraw[:, S_X1, :, :], in_=W1[C0:C0 + C1, :].rearrange("(p j) o -> p j o", j=4))
         nc.sync.dma_start(out=wraw[:, S_X0, 0:2, :], in_=W1[0:C0, :].rearrange("(p e) o -> p e o", e=2))
@@ -130,16 +133,17 @@ def tile_differentiablelogicmachine_pb_t_kernel(tc, x0, x1, x2, W1, b1, out):
             t = UNITS[u][3][k]
             return xt[UNITS[u][0]], t[0], t[-1], UNITS[u][1]
 
-        def a1(u, k, a, b):
+        def a1(u, k, a, b, e0=0, e1=7):
             x, lo, hi, i0 = rows(u, k)
-            if a == lo:
-                m1s[(u, k)] = work.tile([P, hi - lo, 7, C2], BF16, name="m1", tag="m1")
+            if (u, k) not in m1s:
+                tag = "m1" if hi - lo == 4 or u > 0 else "m0"
+                m1s[(u, k)] = work.tile([P, hi - lo, 7, C2], BF16, name=tag, tag=tag)
             m1 = m1s[(u, k)]
-            tt(out=m1[:, a - lo:b - lo], in0=x[:, a:b, 0:7, :], in1=x[:, a:b, 8:15, :], op=ALU.max)
+            tt(out=m1[:, a - lo:b - lo, e0:e1], in0=x[:, a:b, e0:e1, :], in1=x[:, a:b, 8 + e0:8 + e1, :], op=ALU.max)
 
-        def a2(u, a, b):
+        def a2(u, a, b, e0=0, e1=7):
             x = xt[UNITS[u][0]]
-            tt(out=x[:, a:b, 0:7, :], in0=x[:, a:b, 0:7, :], in1=x[:, a:b, 8:15, :], op=ALU.min)
+            tt(out=x[:, a:b, e0:e1, :], in0=x[:, a:b, e0:e1, :], in1=x[:, a:b, 8 + e0:8 + e1, :], op=ALU.min)
 
         def level1(u):
             a, b = UNITS[u][1], UNITS[u][1] + UNITS[u][2]
@@ -265,22 +269,23 @@ def tile_differentiablelogicmachine_pb_t_kernel(tc, x0, x1, x2, W1, b1, out):
                 scl = x1cs[v][1][:, lo:lo + ncol]
             elif kind == 1:
                 slot = S_X0
-                cod = x0cod[:, h * REP * P:h * REP * P + ncol]
-                scl = x0scl[:, h * REP * P:h * REP * P + ncol]
+                cod = x0cod[:, h * P:(h + 1) * P]
+                scl = x0scl[:, h * P:(h + 1) * P]
             else:
                 slot = S_LO + par
                 cod = tcs[u][0][:]
                 scl = tcs[u][1][:]
             cols = slice(slot * O1 + oh * P, slot * O1 + (oh + 1) * P)
-            nc.tensor.matmul_mx(
-                out=accs[(u, oh)][:, par, :],
-                lhsT=wcod[:, cols].bitcast(FP8X4),
-                lhsT_scale=wscl[:, cols],
-                rhs=cod.bitcast(FP8X4),
-                rhs_scale=scl,
-                start=(kind == 0),
-                stop=(kind == 2),
-            )
+            for lo in range(0, ncol, P) if kind == 1 else (0,):
+                nc.tensor.matmul_mx(
+                    out=accs[(u, oh)][:, par, lo:lo + (P if kind == 1 else ncol)],
+                    lhsT=wcod[:, cols].bitcast(FP8X4),
+                    lhsT_scale=wscl[:, cols],
+                    rhs=cod.bitcast(FP8X4),
+                    rhs_scale=scl,
+                    start=(kind == 0),
+                    stop=(kind == 2),
+                )
 
         def mx(u):
             npr = UNITS[u][2] // 2
@@ -309,7 +314,7 @@ def tile_differentiablelogicmachine_pb_t_kernel(tc, x0, x1, x2, W1, b1, out):
                 cod, scl = x1cs[v][0][:, lo:lo + P], x1cs[v][1][:, lo:lo + P]
             elif kind == 1:
                 slot = S_X0
-                cod, scl = x0cod[:, h * REP * P:h * REP * P + P], x0scl[:, h * REP * P:h * REP * P + P]
+                cod, scl = x0cod[:, h * P:(h + 1) * P], x0scl[:, h * P:(h + 1) * P]
             else:
                 slot = S_LO + par
                 cod, scl = tcs[u][0][:], tcs[u][1][:]
@@ -338,11 +343,11 @@ def tile_differentiablelogicmachine_pb_t_kernel(tc, x0, x1, x2, W1, b1, out):
             tt(out=o[:, par, :], in0=accs[(u, par)][:], in1=bbc[:], op=ALU.add)
             nc.scalar.activation(out=o[:, par, :], in_=o[:, par, :], func=ACTF.Sigmoid)
 
-        def last_store(u):
-            h, i0, nr = UNITS[u][0:3]
-            nc.sync.dma_start(out=out[h * P:(h + 1) * P, i0:i0 + nr, :], in_=osbs[u][:])
+        def last_store(u, par):
+            h, i0 = UNITS[u][0:2]
+            nc.sync.dma_start(out=out[h * P:(h + 1) * P, i0 + par, :], in_=osbs[u][:, par, :])
 
-        def fin(u):
+        def fin(u, queue=nc.scalar):
             h, i0, nr = UNITS[u][0:3]
             o = outp.tile([P, nr, O1], F32, name="osb", tag="osb")
             for pr in range(nr // 2):
@@ -354,7 +359,7 @@ def tile_differentiablelogicmachine_pb_t_kernel(tc, x0, x1, x2, W1, b1, out):
                     out=o[:, 2 * pr:2 * pr + 2, :].rearrange("p i o -> p (i o)"),
                     in_=bank[:].rearrange("p a h o -> p (a h o)"),
                 )
-            nc.scalar.dma_start(out=out[h * P:(h + 1) * P, i0:i0 + nr, :], in_=o[:])
+            queue.dma_start(out=out[h * P:(h + 1) * P, i0:i0 + nr, :], in_=o[:])
 
         for s in range(4):
             nc.scalar.copy(out=wgrp[:, s], in_=wraw[:, s].rearrange("p j o -> p o j"))
@@ -364,8 +369,7 @@ def tile_differentiablelogicmachine_pb_t_kernel(tc, x0, x1, x2, W1, b1, out):
         p0 = ps_ot.tile([P, 2, P], F32, name="p0", tag="ot")
         for h in range(2):
             nc.tensor.transpose(p0[:, h, :], x0sb[:, h, :].bitcast(F32), idf[:])
-        for rep in range(REP):
-            nc.scalar.copy(out=g0[:, :, rep, :, 0], in_=p0[:])
+        nc.scalar.copy(out=g0[:, :, :, 0], in_=p0[:])
 
         for u in range(2):
             tx1(u)
@@ -393,21 +397,21 @@ def tile_differentiablelogicmachine_pb_t_kernel(tc, x0, x1, x2, W1, b1, out):
             nc.vector.quantize_mx(
                 out=x0cod[:].bitcast(FP8X4),
                 scales=x0scl[:],
-                in_=g0[:].rearrange("p h r b w -> p (h r b w)").bitcast(BF16),
+                in_=g0[:].rearrange("p h b w -> p (h b w)").bitcast(BF16),
             )
 
-        a1(0, 0, 0, 1)
-        a1(0, 0, 1, 2)
-        a2(0, 0, 1)
-        a2(0, 1, 2)
+        a1(0, 0, 0, 1, 0, 4)
+        a1(0, 0, 0, 1, 4, 7)
+        a2(0, 0, 1, 0, 4)
+        a2(0, 0, 1, 4, 7)
         c(0, 0)
         bb1(0, 0)
         zn(0, 0)
         zx(0, 0)
-        a1(0, 1, 2, 4)
+        a1(0, 1, 1, 2)
         bb2(0, 0)
         d1(0, 0)
-        a2(0, 2, 4)
+        a2(0, 1, 2)
         d2(0, 0)
         c(0, 1)
         e1(0, 0)
@@ -415,18 +419,28 @@ def tile_differentiablelogicmachine_pb_t_kernel(tc, x0, x1, x2, W1, b1, out):
         e2(0, 0)
         zn(0, 1)
         zx(0, 1)
-        a1(1, 0, 4, 6)
+        a1(0, 2, 2, 4)
         bb2(0, 1)
         d1(0, 1)
-        a2(1, 4, 6)
+        a2(0, 2, 4)
         d2(0, 1)
+        c(0, 2)
         e1(0, 1)
-        a1(1, 0, 6, 8)
+        bb1(0, 2)
         e2(0, 1)
+        zn(0, 2)
+        zx(0, 2)
+        a1(1, 0, 4, 6)
+        bb2(0, 2)
+        d1(0, 2)
+        a2(1, 4, 6)
+        d2(0, 2)
+        e1(0, 2)
+        a1(1, 0, 6, 8)
+        e2(0, 2)
         quantize_w()
         a2(1, 6, 8)
         tr(0)
-        ahead(0)
         quantize_x0()
         c(1)
         bb1(1)
@@ -437,14 +451,17 @@ def tile_differentiablelogicmachine_pb_t_kernel(tc, x0, x1, x2, W1, b1, out):
         d1(1)
         d2(1)
         qx1(1)
-        e1(1)
-        e2(1)
         mx(0)
 
         for u in range(1, NU - 3):
-            level1(u + 1)
+            a1(u + 1, 0, UNITS[u + 1][1], UNITS[u + 1][1] + 4)
+            e1(u)
+            e2(u)
+            a2(u + 1, UNITS[u + 1][1], UNITS[u + 1][1] + 4)
             relu(u)
             tr(u)
+            if u == 1:
+                ahead(0)
             fin(u - 1)
             ahead(u)
             c(u + 1)
@@ -453,15 +470,16 @@ def tile_differentiablelogicmachine_pb_t_kernel(tc, x0, x1, x2, W1, b1, out):
             qr(u)
             bb2(u + 1)
             d1(u + 1)
-            d2(u + 1)
             if u + 1 < NX - 1:
                 qx1(u + 1)
-            e1(u + 1)
-            e2(u + 1)
+            d2(u + 1)
             mx(u)
 
         uz, ua, ub = NU - 3, NU - 2, NU - 1
-        level1(ua)
+        a1(ua, 0, 12, 14)
+        e1(uz)
+        e2(uz)
+        a2(ua, 12, 14)
         relu(uz)
         tr(uz)
         fin(uz - 1)
@@ -489,7 +507,7 @@ def tile_differentiablelogicmachine_pb_t_kernel(tc, x0, x1, x2, W1, b1, out):
         e1(ub)
         e2(ub)
         last_open(ub, ps_tx, "tx")
-        fin(uz)
+        fin(uz, nc.sync)
         last_open(ua, ps_acc, "acc")
         tr(ub)
         qr(ua)
@@ -506,4 +524,4 @@ def tile_differentiablelogicmachine_pb_t_kernel(tc, x0, x1, x2, W1, b1, out):
         for u in (ua, ub):
             for par in range(2):
                 last_out(u, par)
-            last_store(u)
+                last_store(u, par)

@@ -49,6 +49,7 @@ def tile_differentiablelogicmachine_pb_t_kernel(tc, x0, x1, x2, W1, b1, out):
         big = ctx.enter_context(tc.tile_pool(name="big", bufs=1))
         x1p = ctx.enter_context(tc.tile_pool(name="x1p", bufs=4))
         work = ctx.enter_context(tc.tile_pool(name="work", bufs=2))
+        fillp = ctx.enter_context(tc.tile_pool(name="fillp", bufs=2))
         outp = ctx.enter_context(tc.tile_pool(name="outp", bufs=3))
         ps_tx = ctx.enter_context(tc.psum_pool(name="ps_tx", bufs=2))
         ps_tr = ctx.enter_context(tc.psum_pool(name="ps_tr", bufs=2))
@@ -133,11 +134,13 @@ def tile_differentiablelogicmachine_pb_t_kernel(tc, x0, x1, x2, W1, b1, out):
             t = UNITS[u][3][k]
             return xt[UNITS[u][0]], t[0], t[-1], UNITS[u][1]
 
+        def new_m1(u, k):
+            x, a, b, i0 = rows(u, k)
+            tag = "m1" if 0 < u < NU - 2 or k == 2 else "m0"
+            m1s[(u, k)] = work.tile([P, b - a, 8, C2], BF16, name=tag, tag=tag)
+
         def a1(u, k, a, b, e0=0, e1=7):
             x, lo, hi, i0 = rows(u, k)
-            if (u, k) not in m1s:
-                tag = "m1" if hi - lo == 4 or u > 0 else "m0"
-                m1s[(u, k)] = work.tile([P, hi - lo, 7, C2], BF16, name=tag, tag=tag)
             m1 = m1s[(u, k)]
             tt(out=m1[:, a - lo:b - lo, e0:e1], in0=x[:, a:b, e0:e1, :], in1=x[:, a:b, 8 + e0:8 + e1, :], op=ALU.max)
 
@@ -153,22 +156,25 @@ def tile_differentiablelogicmachine_pb_t_kernel(tc, x0, x1, x2, W1, b1, out):
             a2(u, a, m)
             a2(u, m, b)
 
-        def c(u, k=0):
+        def fills(u, k=0):
             x, a, b, i0 = rows(u, k)
-            m1 = m1s[(u, k)]
-            tt(out=m1[:, :, 6, :], in0=m1[:, :, 6, :], in1=x[:, a:b, 7, :], op=ALU.max)
+            new_m1(u, k)
+            t = fillp.tile([P, b - a, C2], F32, name="t", tag="t")
+            nc.scalar.activation(out=m1s[(u, k)][:, :, 7, :], in_=x[:, a:b, 7, :], func=ACTF.Relu)
+            nc.scalar.activation(out=t[:], in_=x[:, a:b, 7, :], func=ACTF.Relu, bias=1.0, scale=-1.0)
+            nc.scalar.activation(out=x[:, a:b, 7, :], in_=t[:], func=ACTF.Identity, bias=1.0, scale=-1.0)
+
+        def fill_max(u):
+            x, a, b, i0 = rows(u, 0)
+            nc.vector.tensor_scalar_max(out=m1s[(u, 0)][:, :, 7, :], in0=x[:, a:b, 7, :], scalar1=0.0)
+
+        def fill_min(u):
+            x, a, b, i0 = rows(u, 0)
+            nc.vector.tensor_scalar_min(out=x[:, a:b, 7, :], in0=x[:, a:b, 7, :], scalar1=1.0)
 
         def bb1(u, k=0):
             m1 = m1s[(u, k)]
-            tt(out=m1[:, :, 0:3, :], in0=m1[:, :, 0:3, :], in1=m1[:, :, 3:6, :], op=ALU.max)
-
-        def zn(u, k=0):
-            x, a, b, i0 = rows(u, k)
-            nc.vector.tensor_scalar_min(out=x[:, a:b, 7, :], in0=x[:, a:b, 7, :], scalar1=1.0)
-
-        def zx(u, k=0):
-            m1 = m1s[(u, k)]
-            nc.vector.tensor_scalar_max(out=m1[:, :, 6, :], in0=m1[:, :, 6, :], scalar1=0.0)
+            tt(out=m1[:, :, 0:4, :], in0=m1[:, :, 0:4, :], in1=m1[:, :, 4:8, :], op=ALU.max)
 
         def bb2(u, k=0):
             x, a, b, i0 = rows(u, k)
@@ -176,7 +182,7 @@ def tile_differentiablelogicmachine_pb_t_kernel(tc, x0, x1, x2, W1, b1, out):
 
         def d1(u, k=0):
             m1 = m1s[(u, k)]
-            tt(out=m1[:, :, 0:2, :], in0=m1[:, :, 0:2, :], in1=m1[:, :, 2:7:4, :], op=ALU.max)
+            tt(out=m1[:, :, 0:2, :], in0=m1[:, :, 0:2, :], in1=m1[:, :, 2:4, :], op=ALU.max)
 
         def d2(u, k=0):
             x, a, b, i0 = rows(u, k)
@@ -193,10 +199,6 @@ def tile_differentiablelogicmachine_pb_t_kernel(tc, x0, x1, x2, W1, b1, out):
         def e2(u, k=0):
             x, a, b, i0 = rows(u, k)
             tt(out=rmin[u][:, a - i0:b - i0, :], in0=x[:, a:b, 0, :], in1=x[:, a:b, 1, :], op=ALU.min)
-
-        def relu(u):
-            flat = rmax[u][:].rearrange("p i c -> p (i c)")
-            nc.scalar.activation(out=flat, in_=flat, func=ACTF.Relu)
 
         g1s, x1cs = {}, {}
 
@@ -361,6 +363,8 @@ def tile_differentiablelogicmachine_pb_t_kernel(tc, x0, x1, x2, W1, b1, out):
                 )
             queue.dma_start(out=out[h * P:(h + 1) * P, i0:i0 + nr, :], in_=o[:])
 
+        for k in range(3):
+            fills(0, k)
         for s in range(4):
             nc.scalar.copy(out=wgrp[:, s], in_=wraw[:, s].rearrange("p j o -> p o j"))
         pb = ps_ot.tile([P, P], BF16, name="pb", tag="ot")
@@ -404,32 +408,24 @@ def tile_differentiablelogicmachine_pb_t_kernel(tc, x0, x1, x2, W1, b1, out):
         a1(0, 0, 0, 1, 4, 7)
         a2(0, 0, 1, 0, 4)
         a2(0, 0, 1, 4, 7)
-        c(0, 0)
         bb1(0, 0)
-        zn(0, 0)
-        zx(0, 0)
         a1(0, 1, 1, 2)
         bb2(0, 0)
         d1(0, 0)
         a2(0, 1, 2)
         d2(0, 0)
-        c(0, 1)
         e1(0, 0)
         bb1(0, 1)
         e2(0, 0)
-        zn(0, 1)
-        zx(0, 1)
         a1(0, 2, 2, 4)
         bb2(0, 1)
         d1(0, 1)
         a2(0, 2, 4)
         d2(0, 1)
-        c(0, 2)
         e1(0, 1)
         bb1(0, 2)
         e2(0, 1)
-        zn(0, 2)
-        zx(0, 2)
+        new_m1(1, 0)
         a1(1, 0, 4, 6)
         bb2(0, 2)
         d1(0, 2)
@@ -441,12 +437,13 @@ def tile_differentiablelogicmachine_pb_t_kernel(tc, x0, x1, x2, W1, b1, out):
         quantize_w()
         a2(1, 6, 8)
         tr(0)
+        fill_max(1)
         quantize_x0()
-        c(1)
         bb1(1)
-        zn(1)
+        fill_min(1)
         qx1(0)
         bb2(1)
+        fills(2)
         qr(0)
         d1(1)
         d2(1)
@@ -458,15 +455,13 @@ def tile_differentiablelogicmachine_pb_t_kernel(tc, x0, x1, x2, W1, b1, out):
             e1(u)
             e2(u)
             a2(u + 1, UNITS[u + 1][1], UNITS[u + 1][1] + 4)
-            relu(u)
             tr(u)
             if u == 1:
                 ahead(0)
             fin(u - 1)
             ahead(u)
-            c(u + 1)
+            fills(u + 2)
             bb1(u + 1)
-            zn(u + 1)
             qr(u)
             bb2(u + 1)
             d1(u + 1)
@@ -480,27 +475,21 @@ def tile_differentiablelogicmachine_pb_t_kernel(tc, x0, x1, x2, W1, b1, out):
         e1(uz)
         e2(uz)
         a2(ua, 12, 14)
-        relu(uz)
         tr(uz)
+        fills(ub)
         fin(uz - 1)
-        c(ua)
         bb1(ua)
-        zn(ua)
-        zx(ua)
         a1(ub, 0, 14, 16)
+        qr(uz)
         bb2(ua)
         d1(ua)
-        qr(uz)
-        d2(ua)
         a2(ub, 14, 16)
+        d2(ua)
         mx(uz)
         e1(ua)
-        c(ub)
         e2(ua)
         tr(ua)
         bb1(ub)
-        zn(ub)
-        zx(ub)
         bb2(ub)
         d1(ub)
         d2(ub)

@@ -39,6 +39,7 @@ NX = (B // P) * (N // XR)
 FLOPS = 2 * B * N * K * O1
 BYTES = 2 * (B * C0 + B * N * C1 + B * N * E * C2 + K * O1 + O1) + 4 * B * N * O1
 
+X1_PAIRS = (2, 4)
 S_X1, S_X0, S_LO, S_HI = 0, 1, 2, 3
 
 
@@ -57,8 +58,8 @@ def tile_differentiablelogicmachine_pb_t_kernel(tc, x0, x1, x2, W1, b1, out):
         ps_ot = ctx.enter_context(tc.psum_pool(name="ps_ot", bufs=2))
         ctx.enter_context(tc.manual_schedule())
 
-        wraw = const.tile([P, 4, 4, O1], BF16, name="wraw", tag="wraw")
-        wgrp = const.tile([P, 4, O1, 4], BF16, name="wgrp", tag="wgrp", align_bytes=64)
+        wraw = work.tile([P, 4, 4, O1], BF16, name="wraw", tag="g1", align_bytes=64)
+        wgrp = work.tile([P, 4, O1, 4], BF16, name="wgrp", tag="g1", align_bytes=64)
         wcod = const.tile([P, 4 * O1], U32, name="wcod", tag="wcod", align_bytes=64)
         wscl = const.tile([P, 4 * O1], U8, name="wscl", tag="wscl", align_bytes=64)
         x0sb = const.tile([P, 2, C0], BF16, name="x0sb", tag="x0sb")
@@ -164,14 +165,6 @@ def tile_differentiablelogicmachine_pb_t_kernel(tc, x0, x1, x2, W1, b1, out):
             nc.scalar.activation(out=t[:], in_=x[:, a:b, 7, :], func=ACTF.Relu, bias=1.0, scale=-1.0)
             nc.scalar.activation(out=x[:, a:b, 7, :], in_=t[:], func=ACTF.Identity, bias=1.0, scale=-1.0)
 
-        def fill_max(u):
-            x, a, b, i0 = rows(u, 0)
-            nc.vector.tensor_scalar_max(out=m1s[(u, 0)][:, :, 7, :], in0=x[:, a:b, 7, :], scalar1=0.0)
-
-        def fill_min(u):
-            x, a, b, i0 = rows(u, 0)
-            nc.vector.tensor_scalar_min(out=x[:, a:b, 7, :], in0=x[:, a:b, 7, :], scalar1=1.0)
-
         def bb1(u, k=0):
             m1 = m1s[(u, k)]
             tt(out=m1[:, :, 0:4, :], in0=m1[:, :, 0:4, :], in1=m1[:, :, 4:8, :], op=ALU.max)
@@ -202,11 +195,15 @@ def tile_differentiablelogicmachine_pb_t_kernel(tc, x0, x1, x2, W1, b1, out):
 
         g1s, x1cs = {}, {}
 
-        def tx1(u):
+        def tx1(v):
             npr = XR // 2
-            words = x1t[u][:].bitcast(F32)
-            g1 = work.tile([P, 2, npr, P, 2], F32, name="g1", tag="g1", align_bytes=64)
-            g1s[u] = g1
+            words = x1t[v][:].bitcast(F32)
+            if v not in g1s:
+                n = 2 if v in X1_PAIRS else 1
+                tile_v = work.tile([P, n, 2, npr, P, 2], F32, name="g1", tag="g1", align_bytes=64)
+                for i in range(n):
+                    g1s[v + i] = (tile_v, i)
+            g1, i = g1s[v]
             for par in range(2):
                 bank = ps_tx.tile([P, npr, 2, P], F32, name="tx", tag="tx")
                 for pr in range(npr):
@@ -217,17 +214,20 @@ def tile_differentiablelogicmachine_pb_t_kernel(tc, x0, x1, x2, W1, b1, out):
                             words[:, il * (C1 // 2) + w:(il + 1) * (C1 // 2):2],
                             idf[:],
                         )
-                nc.scalar.copy(out=g1[:, par], in_=bank[:].rearrange("p r w b -> p r b w"))
+                nc.scalar.copy(out=g1[:, i, par], in_=bank[:].rearrange("p r w b -> p r b w"))
 
-        def qx1(u):
-            ncol = XR // 2 * P
-            cod = work.tile([P, 2 * ncol], U32, name="x1cod", tag="x1cod", align_bytes=64)
-            scl = work.tile([P, 2 * ncol], U8, name="x1scl", tag="x1scl", align_bytes=64)
-            x1cs[u] = (cod, scl)
+        def qx1(v):
+            n = 2 if v in X1_PAIRS else 1
+            ncol = n * XR * P
+            cod = work.tile([P, ncol], U32, name="x1cod", tag="x1cod", align_bytes=64)
+            scl = work.tile([P, ncol], U8, name="x1scl", tag="x1scl", align_bytes=64)
+            for i in range(n):
+                cols = slice(i * XR * P, (i + 1) * XR * P)
+                x1cs[v + i] = (cod[:, cols], scl[:, cols])
             nc.vector.quantize_mx(
                 out=cod[:].bitcast(FP8X4),
                 scales=scl[:],
-                in_=g1s[u][:].rearrange("p a r b w -> p (a r b w)").bitcast(BF16),
+                in_=g1s[v][0][:].rearrange("p n a r b w -> p (n a r b w)").bitcast(BF16),
             )
 
         gts, tcs = {}, {}
@@ -243,6 +243,21 @@ def tile_differentiablelogicmachine_pb_t_kernel(tc, x0, x1, x2, W1, b1, out):
             gt = work.tile([P, npr, P, 2], F32, name="gt", tag="gt", align_bytes=64)
             gts[u] = gt
             nc.scalar.copy(out=gt[:], in_=bank[:].rearrange("p r w b -> p r b w"))
+
+        banks = {}
+
+        def tr_pe(u):
+            bank = ps_tr.tile([P, 1, 2, P], F32, name="trb", tag="trb")
+            srcs = (rmax[u], rmin[u])
+            for w in range(2):
+                words = srcs[w][:].rearrange("p i c -> p (i c)").bitcast(F32)
+                nc.tensor.transpose(bank[:, 0, w, :], words[:, 0:P], idf[:])
+            banks[u] = bank
+
+        def tr_copy(u):
+            gt = work.tile([P, 1, P, 2], F32, name="gt", tag="gt", align_bytes=64)
+            gts[u] = gt
+            nc.vector.tensor_copy(out=gt[:], in_=banks[u][:].rearrange("p r w b -> p r b w"))
 
         def qr(u):
             ncol = UNITS[u][2] // 2 * P
@@ -349,7 +364,7 @@ def tile_differentiablelogicmachine_pb_t_kernel(tc, x0, x1, x2, W1, b1, out):
             h, i0 = UNITS[u][0:2]
             nc.sync.dma_start(out=out[h * P:(h + 1) * P, i0 + par, :], in_=osbs[u][:, par, :])
 
-        def fin(u, queue=nc.scalar):
+        def fin(u):
             h, i0, nr = UNITS[u][0:3]
             o = outp.tile([P, nr, O1], F32, name="osb", tag="osb")
             for pr in range(nr // 2):
@@ -361,7 +376,7 @@ def tile_differentiablelogicmachine_pb_t_kernel(tc, x0, x1, x2, W1, b1, out):
                     out=o[:, 2 * pr:2 * pr + 2, :].rearrange("p i o -> p (i o)"),
                     in_=bank[:].rearrange("p a h o -> p (a h o)"),
                 )
-            queue.dma_start(out=out[h * P:(h + 1) * P, i0:i0 + nr, :], in_=o[:])
+            nc.sync.dma_start(out=out[h * P:(h + 1) * P, i0:i0 + nr, :], in_=o[:])
 
         for k in range(3):
             fills(0, k)
@@ -374,6 +389,7 @@ def tile_differentiablelogicmachine_pb_t_kernel(tc, x0, x1, x2, W1, b1, out):
         for h in range(2):
             nc.tensor.transpose(p0[:, h, :], x0sb[:, h, :].bitcast(F32), idf[:])
         nc.scalar.copy(out=g0[:, :, :, 0], in_=p0[:])
+        fills(1)
 
         for u in range(2):
             tx1(u)
@@ -425,7 +441,6 @@ def tile_differentiablelogicmachine_pb_t_kernel(tc, x0, x1, x2, W1, b1, out):
         e1(0, 1)
         bb1(0, 2)
         e2(0, 1)
-        new_m1(1, 0)
         a1(1, 0, 4, 6)
         bb2(0, 2)
         d1(0, 2)
@@ -434,19 +449,17 @@ def tile_differentiablelogicmachine_pb_t_kernel(tc, x0, x1, x2, W1, b1, out):
         e1(0, 2)
         a1(1, 0, 6, 8)
         e2(0, 2)
-        quantize_w()
         a2(1, 6, 8)
+        quantize_w()
         tr(0)
-        fill_max(1)
         quantize_x0()
         bb1(1)
-        fill_min(1)
-        qx1(0)
         bb2(1)
+        qx1(0)
         fills(2)
-        qr(0)
         d1(1)
         d2(1)
+        qr(0)
         qx1(1)
         mx(0)
 
@@ -463,9 +476,11 @@ def tile_differentiablelogicmachine_pb_t_kernel(tc, x0, x1, x2, W1, b1, out):
             fills(u + 2)
             bb1(u + 1)
             qr(u)
+            if u in X1_PAIRS:
+                qx1(u)
             bb2(u + 1)
             d1(u + 1)
-            if u + 1 < NX - 1:
+            if u + 1 == NX - 2:
                 qx1(u + 1)
             d2(u + 1)
             mx(u)
@@ -496,11 +511,12 @@ def tile_differentiablelogicmachine_pb_t_kernel(tc, x0, x1, x2, W1, b1, out):
         e1(ub)
         e2(ub)
         last_open(ub, ps_tx, "tx")
-        fin(uz, nc.sync)
+        fin(uz)
         last_open(ua, ps_acc, "acc")
-        tr(ub)
+        tr_pe(ub)
         qr(ua)
         qx1(ua)
+        tr_copy(ub)
         for par in range(2):
             last_pass(ua, par, 2)
         for par in range(2):

@@ -391,10 +391,9 @@ def tile_differentiablelogicmachine_pb_t_kernel(tc, x0, x1, x2, W1, b1, out):
         nc.scalar.copy(out=g0[:, :, :, 0], in_=p0[:])
         fills(1)
 
-        for u in range(2):
-            tx1(u)
-            load_x2(u + 4)
-            load_x1(u + 4)
+        tx1(0)
+        load_x2(4)
+        load_x1(4)
 
         def ahead(u):
             if u + 2 < NX:
@@ -460,8 +459,10 @@ def tile_differentiablelogicmachine_pb_t_kernel(tc, x0, x1, x2, W1, b1, out):
         d1(1)
         d2(1)
         qr(0)
-        qx1(1)
         mx(0)
+        tx1(1)
+        load_x2(5)
+        load_x1(5)
 
         for u in range(1, NU - 3):
             a1(u + 1, 0, UNITS[u + 1][1], UNITS[u + 1][1] + 4)
@@ -476,7 +477,7 @@ def tile_differentiablelogicmachine_pb_t_kernel(tc, x0, x1, x2, W1, b1, out):
             fills(u + 2)
             bb1(u + 1)
             qr(u)
-            if u in X1_PAIRS:
+            if u == 1 or u in X1_PAIRS:
                 qx1(u)
             bb2(u + 1)
             d1(u + 1)

from contextlib import ExitStack

import concourse.bass as bass
import concourse.mybir as mybir
import concourse.tile as tile
from concourse.masks import make_identity

F32 = mybir.dt.float32
BF16 = mybir.dt.bfloat16
U32 = mybir.dt.uint32
U8 = mybir.dt.uint8
I32 = mybir.dt.int32
FP8X4 = mybir.dt.float8_e4m3fn_x4
ALU = mybir.AluOpType
ACTF = mybir.ActivationFunctionType

P = 128
B, N, C0, C1, C2, O1 = 256, 16, 256, 512, 128, 256
K = C0 + C1 + 2 * C2
E = N - 1
RUN = N * C2

UNITS = (
    (0, 0, 4, ((0, 1), (1, 2), (2, 4))),
    (0, 4, 4, ((4, 6, 8),)),
    (0, 8, 4, ((8, 12),)),
    (0, 12, 4, ((12, 16),)),
    (1, 0, 4, ((0, 4),)),
    (1, 4, 4, ((4, 8),)),
    (1, 8, 4, ((8, 12),)),
    (1, 12, 2, ((12, 14),)),
    (1, 14, 2, ((14, 16),)),
)
NU = 9
assert len(UNITS) == NU
XR = 4
NX = (B // P) * (N // XR)

FLOPS = 2 * B * N * K * O1
BYTES = 2 * (B * C0 + B * N * C1 + B * N * E * C2 + K * O1 + O1) + 4 * B * N * O1

X1_PAIRS = (2, 4)
S_X1, S_X0, S_LO, S_HI = 0, 1, 2, 3


def tile_differentiablelogicmachine_pb_t_kernel(tc, x0, x1, x2, W1, b1, out):
    nc = tc.nc
    with ExitStack() as ctx:
        const = ctx.enter_context(tc.tile_pool(name="const", bufs=1))
        big = ctx.enter_context(tc.tile_pool(name="big", bufs=1))
        x1p = ctx.enter_context(tc.tile_pool(name="x1p", bufs=4))
        work = ctx.enter_context(tc.tile_pool(name="work", bufs=2))
        fillp = ctx.enter_context(tc.tile_pool(name="fillp", bufs=2))
        outp = ctx.enter_context(tc.tile_pool(name="outp", bufs=3))
        ps_tx = ctx.enter_context(tc.psum_pool(name="ps_tx", bufs=2))
        ps_tr = ctx.enter_context(tc.psum_pool(name="ps_tr", bufs=2))
        ps_acc = ctx.enter_context(tc.psum_pool(name="ps_acc", bufs=2))
        ps_ot = ctx.enter_context(tc.psum_pool(name="ps_ot", bufs=2))
        ctx.enter_context(tc.manual_schedule())

        wraw = work.tile([P, 4, 4, O1], BF16, name="wraw", tag="g1", align_bytes=64)
        wgrp = work.tile([P, 4, O1, 4], BF16, name="wgrp", tag="g1", align_bytes=64)
        wcod = const.tile([P, 4 * O1], U32, name="wcod", tag="wcod", align_bytes=64)
        wscl = const.tile([P, 4 * O1], U8, name="wscl", tag="wscl", align_bytes=64)
        x0sb = const.tile([P, 2, C0], BF16, name="x0sb", tag="x0sb")
        g0 = const.tile([P, 2, P, 2], F32, name="g0", tag="g0", align_bytes=64)
        x0cod = const.tile([P, 2 * P], U32, name="x0cod", tag="x0cod", align_bytes=64)
        x0scl = const.tile([P, 2 * P], U8, name="x0scl", tag="x0scl", align_bytes=64)
        bz = const.tile([P, P], BF16, name="bz", tag="bz")
        bias = const.tile([P, 2], F32, name="bias", tag="bias")
        warm = const.tile([P, 2], F32, name="warm", tag="warm")
        idf = const.tile([P, P], F32, name="idf", tag="idf")
        idb = const.tile([P, P], BF16, name="idb", tag="idb")
        bbc = const.tile([P, O1], BF16, name="bbc", tag="bbc")

        nc.vector.memset(warm[:], 0.0)
        nc.vector.memset(bz[:], 0.0)
        nc.gpsimd.memset(wraw[:, S_X0, 2:4, :], 0.0)
        nc.gpsimd.memset(wraw[64:128, S_LO, :, :], 0.0)
        nc.gpsimd.memset(wraw[0:64, S_HI, :, :], 0.0)
        nc.vector.memset(g0[:], 0.0)
        make_identity(nc, idf[:])
        make_identity(nc, idb[:])
        nc.scalar.activation(out=warm[:, 1:2], in_=warm[:, 0:1], func=ACTF.Sigmoid)

        xt = [big.tile([P, N, E, C2], BF16, name="xt%d" % h, tag="xt%d" % h) for h in range(2)]

        def load_x2(u, steps=slice(0, 3)):
            h = UNITS[u][0]
            bounds = [p for t in UNITS[u][3] for p in zip(t[:-1], t[1:])]
            for a, b in bounds[steps]:
                g_lo = (E * a + N - 1) // N
                g_hi = (E * b + N - 1) // N
                src = x2[h * P:(h + 1) * P].rearrange("b i j c -> b (i j c)")[:, C2:N * N * C2]
                src = src.rearrange("b (g r) -> b g r", r=RUN + C2)[:, g_lo:g_hi, 0:RUN]
                dst = xt[h][:].rearrange("p i e c -> p (i e c)")[:, g_lo * RUN:g_hi * RUN]
                nc.sync.dma_start(out=dst.rearrange("p (g r) -> p g r", r=RUN), in_=src)

        x1t = {}

        def load_x1(v):
            h, q = divmod(v, N // XR)
            t = x1p.tile([P, XR * C1], BF16, name="x1t", tag="x1t")
            nc.sync.dma_start(
                out=t[:].rearrange("p (i k) -> p i k", k=C1),
                in_=x1[h * P:(h + 1) * P, q * XR:(q + 1) * XR, :],
            )
            x1t[v] = t

        first = x2[0:P].rearrange("b i j c -> b (i j c)")[:, C2:C2 + RUN].rearrange("b (s e c) -> b s (e c)", s=2, c=C2)
        row0 = xt[0][:].rearrange("p i e c -> p (i e c)")[:, 0:RUN].rearrange("p (s f) -> p s f", s=2)
        for lo, hi in ((0, 4), (4, 8)):
            nc.sync.dma_start(out=row0[:, :, lo * C2:hi * C2], in_=first[:, :, lo * C2:hi * C2])
        load_x2(0, slice(1, 3))
        load_x2(1, slice(0, 1))
        nc.sync.dma_start(out=wraw[:, S_X1, :, :], in_=W1[C0:C0 + C1, :].rearrange("(p j) o -> p j o", j=4))
        nc.sync.dma_start(out=wraw[:, S_X0, 0:2, :], in_=W1[0:C0, :].rearrange("(p e) o -> p e o", e=2))
        wr_src = W1[C0 + C1:K, :].rearrange("(u p e) o -> p u (e o)", u=2, e=2)
        nc.sync.dma_start(out=wraw[0:64, S_LO, :, :].rearrange("p (u e) o -> p u (e o)", u=2), in_=wr_src)
        nc.sync.dma_start(out=wraw[64:128, S_HI, :, :].rearrange("p (u e) o -> p u (e o)", u=2), in_=wr_src)
        load_x2(1, slice(1, 2))
        nc.sync.dma_start(out=x0sb[:], in_=x0.rearrange("(h b) k -> b h k", h=2))
        nc.sync.dma_start(out=bz[0:2, :], in_=b1.rearrange("(r c) -> r c", r=2))
        load_x1(0)
        load_x1(1)
        load_x2(2)
        load_x1(2)
        load_x2(3)
        load_x1(3)

        rmax, rmin, m1s = {}, {}, {}
        tt = nc.vector.tensor_tensor

        def rows(u, k):
            t = UNITS[u][3][k]
            return xt[UNITS[u][0]], t[0], t[-1], UNITS[u][1]

        def new_m1(u, k):
            x, a, b, i0 = rows(u, k)
            tag = "m1" if 0 < u < NU - 2 or k == 2 else "m0"
            m1s[(u, k)] = work.tile([P, b - a, 8, C2], BF16, name=tag, tag=tag)

        def a1(u, k, a, b, e0=0, e1=7):
            x, lo, hi, i0 = rows(u, k)
            m1 = m1s[(u, k)]
            tt(out=m1[:, a - lo:b - lo, e0:e1], in0=x[:, a:b, e0:e1, :], in1=x[:, a:b, 8 + e0:8 + e1, :], op=ALU.max)

        def a2(u, a, b, e0=0, e1=7):
            x = xt[UNITS[u][0]]
            tt(out=x[:, a:b, e0:e1, :], in0=x[:, a:b, e0:e1, :], in1=x[:, a:b, 8 + e0:8 + e1, :], op=ALU.min)

        def level1(u):
            a, b = UNITS[u][1], UNITS[u][1] + UNITS[u][2]
            m = (a + b) // 2
            a1(u, 0, a, m)
            a1(u, 0, m, b)
            a2(u, a, m)
            a2(u, m, b)

        def fills(u, k=0):
            x, a, b, i0 = rows(u, k)
            new_m1(u, k)
            t = fillp.tile([P, b - a, C2], F32, name="t", tag="t")
            nc.scalar.activation(out=m1s[(u, k)][:, :, 7, :], in_=x[:, a:b, 7, :], func=ACTF.Relu)
            nc.scalar.activation(out=t[:], in_=x[:, a:b, 7, :], func=ACTF.Relu, bias=1.0, scale=-1.0)
            nc.scalar.activation(out=x[:, a:b, 7, :], in_=t[:], func=ACTF.Identity, bias=1.0, scale=-1.0)

        def bb1(u, k=0):
            m1 = m1s[(u, k)]
            tt(out=m1[:, :, 0:4, :], in0=m1[:, :, 0:4, :], in1=m1[:, :, 4:8, :], op=ALU.max)

        def bb2(u, k=0):
            x, a, b, i0 = rows(u, k)
            tt(out=x[:, a:b, 0:4, :], in0=x[:, a:b, 0:4, :], in1=x[:, a:b, 4:8, :], op=ALU.min)

        def d1(u, k=0):
            m1 = m1s[(u, k)]
            tt(out=m1[:, :, 0:2, :], in0=m1[:, :, 0:2, :], in1=m1[:, :, 2:4, :], op=ALU.max)

        def d2(u, k=0):
            x, a, b, i0 = rows(u, k)
            tt(out=x[:, a:b, 0:2, :], in0=x[:, a:b, 0:2, :], in1=x[:, a:b, 2:4, :], op=ALU.min)

        def e1(u, k=0):
            x, a, b, i0 = rows(u, k)
            if k == 0:
                rmax[u] = work.tile([P, UNITS[u][2], C2], BF16, name="rx", tag="rx")
                rmin[u] = work.tile([P, UNITS[u][2], C2], BF16, name="rn", tag="rn")
            m1 = m1s[(u, k)]
            tt(out=rmax[u][:, a - i0:b - i0, :], in0=m1[:, :, 0, :], in1=m1[:, :, 1, :], op=ALU.max)

        def e2(u, k=0):
            x, a, b, i0 = rows(u, k)
            tt(out=rmin[u][:, a - i0:b - i0, :], in0=x[:, a:b, 0, :], in1=x[:, a:b, 1, :], op=ALU.min)

        g1s, x1cs = {}, {}

        def tx1(v):
            npr = XR // 2
            words = x1t[v][:].bitcast(F32)
            if v not in g1s:
                n = 2 if v in X1_PAIRS else 1
                tile_v = work.tile([P, n, 2, npr, P, 2], F32, name="g1", tag="g1", align_bytes=64)
                for i in range(n):
                    g1s[v + i] = (tile_v, i)
            g1, i = g1s[v]
            for par in range(2):
                bank = ps_tx.tile([P, npr, 2, P], F32, name="tx", tag="tx")
                for pr in range(npr):
                    il = 2 * pr + par
                    for w in range(2):
                        nc.tensor.transpose(
                            bank[:, pr, w, :],
                            words[:, il * (C1 // 2) + w:(il + 1) * (C1 // 2):2],
                            idf[:],
                        )
                nc.scalar.copy(out=g1[:, i, par], in_=bank[:].rearrange("p r w b -> p r b w"))

        def qx1(v):
            n = 2 if v in X1_PAIRS else 1
            ncol = n * XR * P
            cod = work.tile([P, ncol], U32, name="x1cod", tag="x1cod", align_bytes=64)
            scl = work.tile([P, ncol], U8, name="x1scl", tag="x1scl", align_bytes=64)
            for i in range(n):
                cols = slice(i * XR * P, (i + 1) * XR * P)
                x1cs[v + i] = (cod[:, cols], scl[:, cols])
            nc.vector.quantize_mx(
                out=cod[:].bitcast(FP8X4),
                scales=scl[:],
                in_=g1s[v][0][:].rearrange("p n a r b w -> p (n a r b w)").bitcast(BF16),
            )

        gts, tcs = {}, {}

        def tr(u):
            npr = UNITS[u][2] // 2
            bank = ps_tr.tile([P, npr, 2, P], F32, name="trb", tag="trb")
            srcs = (rmax[u], rmin[u])
            for pr in range(npr):
                for w in range(2):
                    words = srcs[w][:].rearrange("p i c -> p (i c)").bitcast(F32)
                    nc.tensor.transpose(bank[:, pr, w, :], words[:, pr * P:(pr + 1) * P], idf[:])
            gt = work.tile([P, npr, P, 2], F32, name="gt", tag="gt", align_bytes=64)
            gts[u] = gt
            nc.scalar.copy(out=gt[:], in_=bank[:].rearrange("p r w b -> p r b w"))

        banks = {}

        def tr_pe(u):
            bank = ps_tr.tile([P, 1, 2, P], F32, name="trb", tag="trb")
            srcs = (rmax[u], rmin[u])
            for w in range(2):
                words = srcs[w][:].rearrange("p i c -> p (i c)").bitcast(F32)
                nc.tensor.transpose(bank[:, 0, w, :], words[:, 0:P], idf[:])
            banks[u] = bank

        def tr_copy(u):
            gt = work.tile([P, 1, P, 2], F32, name="gt", tag="gt", align_bytes=64)
            gts[u] = gt
            nc.vector.tensor_copy(out=gt[:], in_=banks[u][:].rearrange("p r w b -> p r b w"))

        def qr(u):
            ncol = UNITS[u][2] // 2 * P
            cod = work.tile([P, ncol], U32, name="rcod", tag="rcod", align_bytes=64)
            scl = work.tile([P, ncol], U8, name="rscl", tag="rscl", align_bytes=64)
            tcs[u] = (cod, scl)
            nc.vector.quantize_mx(
                out=cod[:].bitcast(FP8X4),
                scales=scl[:],
                in_=gts[u][:].rearrange("p r b w -> p (r b w)").bitcast(BF16),
            )

        sig, accs = {}, {}

        def x1_cols(u, par):
            h, i0 = UNITS[u][0:2]
            return h * (N // XR) + i0 // XR, (par * (XR // 2) + (i0 % XR) // 2) * P

        def mx_pass(u, oh, par, kind):
            h = UNITS[u][0]
            ncol = UNITS[u][2] // 2 * P
            if kind == 0:
                slot = S_X1
                v, lo = x1_cols(u, par)
                cod = x1cs[v][0][:, lo:lo + ncol]
                scl = x1cs[v][1][:, lo:lo + ncol]
            elif kind == 1:
                slot = S_X0
                cod = x0cod[:, h * P:(h + 1) * P]
                scl = x0scl[:, h * P:(h + 1) * P]
            else:
                slot = S_LO + par
                cod = tcs[u][0][:]
                scl = tcs[u][1][:]
            cols = slice(slot * O1 + oh * P, slot * O1 + (oh + 1) * P)
            for lo in range(0, ncol, P) if kind == 1 else (0,):
                nc.tensor.matmul_mx(
                    out=accs[(u, oh)][:, par, lo:lo + (P if kind == 1 else ncol)],
                    lhsT=wcod[:, cols].bitcast(FP8X4),
                    lhsT_scale=wscl[:, cols],
                    rhs=cod.bitcast(FP8X4),
                    rhs_scale=scl,
                    start=(kind == 0),
                    stop=(kind == 2),
                )

        def mx(u):
            npr = UNITS[u][2] // 2
            for oh in range(2):
                accs[(u, oh)] = ps_acc.tile([P, 2, npr * P], F32, name="acc", tag="acc")
            for par in range(2):
                for kind in range(3):
                    for oh in range(2):
                        mx_pass(u, oh, par, kind)
            for oh in range(2):
                s = work.tile([P, 2, npr, P], F32, name="sig%d" % oh, tag="sig%d" % oh)
                sig[(u, oh)] = s
                nc.scalar.activation(
                    out=s[:].rearrange("p a r b -> p (a r b)"),
                    in_=accs[(u, oh)][:].rearrange("p a n -> p (a n)"),
                    func=ACTF.Sigmoid,
                    bias=bias[:, oh:oh + 1],
                    scale=1.0,
                )

        def last_pass(u, par, kind, start=False, stop=False):
            h = UNITS[u][0]
            if kind == 0:
                slot = S_X1
                v, lo = x1_cols(u, par)
                cod, scl = x1cs[v][0][:, lo:lo + P], x1cs[v][1][:, lo:lo + P]
            elif kind == 1:
                slot = S_X0
                cod, scl = x0cod[:, h * P:(h + 1) * P], x0scl[:, h * P:(h + 1) * P]
            else:
                slot = S_LO + par
                cod, scl = tcs[u][0][:], tcs[u][1][:]
            cols = slice(slot * O1, (slot + 1) * O1)
            nc.tensor.matmul_mx(
                out=accs[(u, par)][:],
                lhsT=cod.bitcast(FP8X4),
                lhsT_scale=scl,
                rhs=wcod[:, cols].bitcast(FP8X4),
                rhs_scale=wscl[:, cols],
                start=start,
                stop=stop,
            )

        osbs = {}

        def last_open(u, pool, tag):
            nr = UNITS[u][2]
            osbs[u] = work.tile([P, nr, O1], F32, name="olast", tag="olast")
            for par in range(2):
                accs[(u, par)] = pool.tile([P, O1], F32, name=tag, tag=tag)
                last_pass(u, par, 1, start=True)

        def last_out(u, par):
            o = osbs[u]
            tt(out=o[:, par, :], in0=accs[(u, par)][:], in1=bbc[:], op=ALU.add)
            nc.scalar.activation(out=o[:, par, :], in_=o[:, par, :], func=ACTF.Sigmoid)

        def last_store(u, par):
            h, i0 = UNITS[u][0:2]
            nc.sync.dma_start(out=out[h * P:(h + 1) * P, i0 + par, :], in_=osbs[u][:, par, :])

        def fin(u):
            h, i0, nr = UNITS[u][0:3]
            o = outp.tile([P, nr, O1], F32, name="osb", tag="osb")
            for pr in range(nr // 2):
                bank = ps_ot.tile([P, 2, 2, P], F32, name="ot", tag="ot")
                for par in range(2):
                    for oh in range(2):
                        nc.tensor.transpose(bank[:, par, oh, :], sig[(u, oh)][:, par, pr, :], idf[:])
                nc.scalar.copy(
                    out=o[:, 2 * pr:2 * pr + 2, :].rearrange("p i o -> p (i o)"),
                    in_=bank[:].rearrange("p a h o -> p (a h o)"),
                )
            nc.sync.dma_start(out=out[h * P:(h + 1) * P, i0:i0 + nr, :], in_=o[:])

        for k in range(3):
            fills(0, k)
        for s in range(4):
            nc.scalar.copy(out=wgrp[:, s], in_=wraw[:, s].rearrange("p j o -> p o j"))
        pb = ps_ot.tile([P, P], BF16, name="pb", tag="ot")
        nc.tensor.transpose(pb[:], bz[:], idb[:])
        nc.scalar.copy(out=bias[:], in_=pb[:, 0:2])
        p0 = ps_ot.tile([P, 2, P], F32, name="p0", tag="ot")
        for h in range(2):
            nc.tensor.transpose(p0[:, h, :], x0sb[:, h, :].bitcast(F32), idf[:])
        nc.scalar.copy(out=g0[:, :, :, 0], in_=p0[:])
        fills(1)

        tx1(0)
        load_x2(4)
        load_x1(4)

        def ahead(u):
            if u + 2 < NX:
                tx1(u + 2)
            if u + 6 < NU:
                load_x2(u + 6)
            if u + 6 < NX:
                load_x1(u + 6)
            if u + 6 == NU:
                nc.sync.dma_start(out=bbc[:], in_=b1.partition_broadcast(P))

        def quantize_w():
            nc.vector.quantize_mx(
                out=wcod[:].bitcast(FP8X4),
                scales=wscl[:],
                in_=wgrp[:].rearrange("p s o j -> p (s o j)"),
            )

        def quantize_x0():
            nc.vector.quantize_mx(
                out=x0cod[:].bitcast(FP8X4),
                scales=x0scl[:],
                in_=g0[:].rearrange("p h b w -> p (h b w)").bitcast(BF16),
            )

        a1(0, 0, 0, 1, 0, 4)
        a1(0, 0, 0, 1, 4, 7)
        a2(0, 0, 1, 0, 4)
        a2(0, 0, 1, 4, 7)
        bb1(0, 0)
        a1(0, 1, 1, 2)
        bb2(0, 0)
        d1(0, 0)
        a2(0, 1, 2)
        d2(0, 0)
        e1(0, 0)
        bb1(0, 1)
        e2(0, 0)
        a1(0, 2, 2, 4)
        bb2(0, 1)
        d1(0, 1)
        a2(0, 2, 4)
        d2(0, 1)
        e1(0, 1)
        bb1(0, 2)
        e2(0, 1)
        a1(1, 0, 4, 6)
        bb2(0, 2)
        d1(0, 2)
        a2(1, 4, 6)
        d2(0, 2)
        e1(0, 2)
        a1(1, 0, 6, 8)
        e2(0, 2)
        a2(1, 6, 8)
        quantize_w()
        tr(0)
        quantize_x0()
        bb1(1)
        bb2(1)
        qx1(0)
        fills(2)
        d1(1)
        d2(1)
        qr(0)
        mx(0)
        tx1(1)
        load_x2(5)
        load_x1(5)

        for u in range(1, NU - 3):
            a1(u + 1, 0, UNITS[u + 1][1], UNITS[u + 1][1] + 4)
            e1(u)
            e2(u)
            a2(u + 1, UNITS[u + 1][1], UNITS[u + 1][1] + 4)
            tr(u)
            if u == 1:
                ahead(0)
            fin(u - 1)
            ahead(u)
            fills(u + 2)
            bb1(u + 1)
            qr(u)
            if u == 1 or u in X1_PAIRS:
                qx1(u)
            bb2(u + 1)
            d1(u + 1)
            if u + 1 == NX - 2:
                qx1(u + 1)
            d2(u + 1)
            mx(u)

        uz, ua, ub = NU - 3, NU - 2, NU - 1
        a1(ua, 0, 12, 14)
        e1(uz)
        e2(uz)
        a2(ua, 12, 14)
        tr(uz)
        fills(ub)
        fin(uz - 1)
        bb1(ua)
        a1(ub, 0, 14, 16)
        qr(uz)
        bb2(ua)
        d1(ua)
        a2(ub, 14, 16)
        d2(ua)
        mx(uz)
        e1(ua)
        e2(ua)
        tr(ua)
        bb1(ub)
        bb2(ub)
        d1(ub)
        d2(ub)
        e1(ub)
        e2(ub)
        last_open(ub, ps_tx, "tx")
        fin(uz)
        last_open(ua, ps_acc, "acc")
        tr_pe(ub)
        qr(ua)
        qx1(ua)
        tr_copy(ub)
        for par in range(2):
            last_pass(ua, par, 2)
        for par in range(2):
            last_pass(ua, par, 0, stop=True)
        for par in range(2):
            last_pass(ub, par, 0)
        qr(ub)
        for par in range(2):
            last_pass(ub, par, 2, stop=True)
        for u in (ua, ub):
            for par in range(2):
                last_out(u, par)
                last_store(u, par)
